import numpy as np
import ml_dtypes


def mxq(x, axis, fmt="e4m3"):
    dtype, down = {"e4m3": (ml_dtypes.float8_e4m3fn, 7), "e5m2": (ml_dtypes.float8_e5m2, 14)}[fmt]
    v = np.moveaxis(np.asarray(x, np.float32).astype(ml_dtypes.bfloat16).astype(np.float64), axis, -1)
    blocks = v.reshape(v.shape[:-1] + (-1, 32))
    amax = np.abs(blocks).max(-1, keepdims=True)
    byte = np.maximum(np.where(amax > 0, np.frexp(amax)[1] - 1 + 127, 0) - down, 1)
    scale = np.exp2(byte - 127.0)
    codes = (blocks / scale).astype(np.float32).astype(dtype).astype(np.float64)
    return np.moveaxis((codes * scale).reshape(v.shape), -1, axis)


WIDE = False


def mx_kscale(k):
    if not WIDE:
        return np.ones(k)
    levels = np.array([10, -10, 5, -5, 0])
    a = np.random.permutation(np.resize(levels, k // 512 * 4)).reshape(k // 512, 4)
    idx = np.arange(k)
    return np.exp2(a[idx // 512, idx % 128 // 32])


BF16 = ml_dtypes.bfloat16


def bf(x):
    return np.asarray(x, np.float32).astype(BF16)


def f64(x):
    return np.asarray(x).astype(np.float64)


B, IN_C, OUT_C, HM, HN, NL = 4096, 512, 256, 1024, 4, 3


def rmsnorm2d(v):
    for d in (-2, -1):
        v = v - v.mean(d, keepdims=True)
        v = v / np.maximum(np.sqrt(np.mean(v * v, d, keepdims=True)), 1e-8)
    return v


def setup_inputs():
    s = mx_kscale(HM)
    g = np.random.standard_normal((B, HN))
    e = np.exp(g - g.max(-1, keepdims=True))
    return {"h_pre": bf(1.5 * np.random.standard_normal((B, HN, HM)) * s),
            "W_mo": bf(np.random.standard_normal((HN, HM, OUT_C)) / np.sqrt(HM) / s[None, :, None]),
            "weights_n": bf(e / e.sum(-1, keepdims=True)),
            "leak_n": bf(np.random.uniform(-2.0, 2.0, HN))}


def reference(h_pre, W_mo, weights_n, leak_n):
    h = f64(h_pre)
    h = np.where(h < 0, h * f64(leak_n)[:, None], h)
    y = (mxq(h, 2, "e4m3").transpose(1, 0, 2) @ mxq(f64(W_mo), 1, "e4m3")).transpose(1, 0, 2)
    y = y * f64(weights_n)[..., None]
    return rmsnorm2d(y).mean(-2)

@@ -1,0 +1,267 @@
+from contextlib import ExitStack
+
+import concourse.mybir as mybir
+from concourse.masks import make_identity
+
+F32 = mybir.dt.float32
+BF16 = mybir.dt.bfloat16
+U32 = mybir.dt.uint32
+U8 = mybir.dt.uint8
+FP8X4 = mybir.dt.float8_e4m3fn_x4
+ALU = mybir.AluOpType
+ACT = mybir.ActivationFunctionType
+AX = mybir.AxisListType
+
+P = 128
+B, HN, HM, OC = 4096, 4, 1024, 256
+NT = B // P
+GROUP = 4
+FLOPS = 2 * B * HN * HM * OC
+
+USE_TACC = True
+LAG = 1
+
+
+def l_on_vector(t, n):
+    return n == 3 and t % 2 == 1
+
+
+def tile_tensormoe_pb_t_kernel(tc, h_pre, W_mo, weights_n, leak_n, out):
+    nc = tc.nc
+    with ExitStack() as ctx:
+        const = ctx.enter_context(tc.tile_pool(name="const", bufs=1))
+        hpool = ctx.enter_context(tc.tile_pool(name="hpool", bufs=4))
+        lpool = ctx.enter_context(tc.tile_pool(name="lpool", bufs=4))
+        gpool = ctx.enter_context(tc.tile_pool(name="gpool", bufs=2))
+        qpool = ctx.enter_context(tc.tile_pool(name="qpool", bufs=2))
+        epool = ctx.enter_context(tc.tile_pool(name="epool", bufs=2))
+        upool = ctx.enter_context(tc.tile_pool(name="upool", bufs=2 * GROUP))
+        spool = ctx.enter_context(tc.tile_pool(name="spool", bufs=2))
+        opool = ctx.enter_context(tc.tile_pool(name="opool", bufs=2))
+        xpsum = ctx.enter_context(tc.psum_pool(name="xpsum", bufs=3))
+        ypsum = ctx.enter_context(tc.psum_pool(name="ypsum", bufs=3))
+        mpsum = ctx.enter_context(tc.psum_pool(name="mpsum", bufs=1))
+
+        h_view = h_pre.rearrange("(p t) n m -> p t (n m)", t=NT)
+        out_view = out.rearrange("(p t) o -> p t o", t=NT)
+
+        lkb = const.tile([P, HN], BF16)
+        nc.sync.dma_start(out=lkb[:], in_=leak_n.partition_broadcast(P))
+        wtb = const.tile([P, NT * HN], BF16)
+        nc.sync.dma_start(out=wtb[:], in_=weights_n.rearrange("(p t) n -> p (t n)", t=NT))
+
+        htiles = {}
+
+        def load(t):
+            hsb = hpool.tile([P, HN * HM], BF16, name="hsb")
+            nc.sync.dma_start(out=hsb[:], in_=h_view[:, t, :])
+            htiles[t] = hsb
+
+        load(0)
+        wraw = const.tile([P, 16 * 512], BF16)
+        nc.sync.dma_start(
+            out=wraw[:].rearrange("p (a r) -> p a r", a=16),
+            in_=W_mo.rearrange("n (g u p e) o -> p (n g u) (e o)", g=2, u=2, p=P, e=2),
+        )
+        load(1)
+        load(2)
+
+        ident = const.tile([P, P], F32)
+        make_identity(nc, ident[:])
+
+        lk = const.tile([P, HN], F32)
+        nc.vector.tensor_copy(out=lk[:], in_=lkb[:])
+        sg = const.tile([P, HN], F32)
+        nc.vector.tensor_scalar(out=sg[:], in0=lk[:], scalar1=1.0, scalar2=-2.0, op0=ALU.is_gt, op1=ALU.mult)
+        nc.vector.tensor_scalar_add(out=sg[:], in0=sg[:], scalar1=1.0)
+        wp = const.tile([P, NT, HN], F32)
+        nc.vector.tensor_tensor(
+            out=wp[:],
+            in0=wtb[:].rearrange("p (t n) -> p t n", n=HN),
+            in1=sg[:].unsqueeze(1).to_broadcast([P, NT, HN]),
+            op=ALU.mult,
+        )
+
+        wgrp = const.tile([P, 8192], BF16, align_bytes=64)
+        wsrc = wraw[:].rearrange("p (a t o) -> p a o t", a=8, t=4, o=OC)
+        wdst = wgrp[:].rearrange("p (a o t) -> p a o t", a=8, t=4, o=OC)
+        nc.vector.tensor_copy(out=wdst[:, 0:4], in_=wsrc[:, 0:4])
+        nc.scalar.copy(out=wdst[:, 4:8], in_=wsrc[:, 4:8])
+        wcodes = const.tile([P, 2048], U32, align_bytes=64)
+        wscales = const.tile([P, 2048], U8, align_bytes=64)
+        for hf in range(2):
+            nc.vector.quantize_mx(
+                out=wcodes[:, hf * 1024 : (hf + 1) * 1024].bitcast(FP8X4),
+                scales=wscales[:, hf * 1024 : (hf + 1) * 1024],
+                in_=wgrp[:, hf * 4096 : (hf + 1) * 4096],
+            )
+
+        su = const.tile([P, NT, HN], F32)
+        sq = const.tile([P, NT, HN], F32)
+
+        ytiles = {}
+        utiles = {}
+
+        def main(t):
+            hsb = htiles.pop(t)
+            for n in range(HN):
+                sl = hsb[:, n * HM : (n + 1) * HM]
+                nc.vector.tensor_scalar(out=sl, in0=sl, scalar1=sg[:, n : n + 1], scalar2=None, op0=ALU.mult)
+            hw = hsb[:].bitcast(F32)
+            grp = gpool.tile([P, HN * HM], BF16, name="grp", align_bytes=64)
+            for n in range(HN):
+                xt = xpsum.tile([P, 512], F32, name="xt")
+                for u in range(2):
+                    for g in range(2):
+                        j = u * 2 + g
+                        c0 = n * 512 + g * 256 + u * 128
+                        nc.tensor.transpose(xt[:, j * P : (j + 1) * P], hw[:, c0 : c0 + P], ident[:])
+                xb = xt[:].bitcast(BF16)
+                lt = lpool.tile([P, HM], BF16, name="lt")
+                if l_on_vector(t, n):
+                    nc.vector.tensor_scalar(out=lt[:], in0=xb, scalar1=lk[:, n : n + 1], scalar2=None, op0=ALU.mult)
+                else:
+                    nc.scalar.activation(out=lt[:], in_=xb, func=ACT.Copy, scale=lk[:, n : n + 1])
+                nc.vector.tensor_tensor(
+                    out=grp[:, n * HM : (n + 1) * HM].rearrange("p (w u e) -> p w u e", u=2, e=2),
+                    in0=lt[:].rearrange("p (u w e) -> p w u e", u=2, e=2),
+                    in1=xb.rearrange("p (u w e) -> p w u e", u=2, e=2),
+                    op=ALU.max,
+                )
+            codes = qpool.tile([P, HN * 256], U32, name="codes", align_bytes=64)
+            scales = qpool.tile([P, HN * 256], U8, name="scales", align_bytes=64)
+            nc.vector.quantize_mx(out=codes[:].bitcast(FP8X4), scales=scales[:], in_=grp[:])
+            ys = []
+            for pr in range(2):
+                y = ypsum.tile([P, 2, OC], F32, name="y")
+                for nn in range(2):
+                    n = pr * 2 + nn
+                    for g in range(2):
+                        a = n * 2 + g
+                        nc.tensor.matmul_mx(
+                            out=y[:, nn, :],
+                            lhsT=codes[:, a * P : (a + 1) * P].bitcast(FP8X4),
+                            lhsT_scale=scales[:, a * P : (a + 1) * P],
+                            rhs=wcodes[:, a * OC : (a + 1) * OC].bitcast(FP8X4),
+                            rhs_scale=wscales[:, a * OC : (a + 1) * OC],
+                            start=(g == 0),
+                            stop=(g == 1),
+                        )
+                ys.append(y)
+            ytiles[t] = ys
+
+        def sum_over_experts(src, tagname):
+            m = mpsum.tile([P, 512], F32, name=tagname)
+            for hf in range(2):
+                for n in range(HN):
+                    nc.tensor.matmul(
+                        out=m[:, hf * P : (hf + 1) * P],
+                        lhsT=src[:, n, hf * P : (hf + 1) * P],
+                        rhs=ident[:],
+                        start=(n == 0),
+                        stop=(n == HN - 1),
+                        is_transpose=True,
+                    )
+            return m
+
+        def back(m, srcT):
+            for hf in range(2):
+                nc.tensor.transpose(m[:, 256 + hf * P : 256 + (hf + 1) * P], srcT[:, hf * P : (hf + 1) * P], ident[:])
+            return m[:, 256:512]
+
+        def epi(t):
+            ys = ytiles.pop(t)
+            z = epool.tile([P, HN, OC], F32, name="z")
+            for n in range(HN):
+                nc.scalar.activation(out=z[:, n, :], in_=ys[n // 2][:, n % 2, :], func=ACT.Copy, scale=wp[:, t, n : n + 1])
+            c = epool.tile([P, HN, OC], F32, name="c")
+            if USE_TACC:
+                mA = sum_over_experts(z, "mA")
+                nmT = spool.tile([P, OC], F32, name="nmT")
+                nc.scalar.activation(out=nmT[:], in_=mA[:, 0:256], func=ACT.Copy, scale=-0.25)
+                nm = back(mA, nmT)
+                nc.vector.tensor_tensor(out=c[:], in0=z[:], in1=nm.unsqueeze(1).to_broadcast([P, HN, OC]), op=ALU.add)
+            else:
+                s2 = spool.tile([P, 2, OC], F32, name="s2")
+                nc.vector.tensor_tensor(out=s2[:], in0=z[:, 0:2, :], in1=z[:, 2:4, :], op=ALU.add)
+                s4 = spool.tile([P, OC], F32, name="s4")
+                nc.vector.tensor_tensor(out=s4[:], in0=s2[:, 0, :], in1=s2[:, 1, :], op=ALU.add)
+                nc.vector.scalar_tensor_tensor(
+                    out=c[:], in0=s4[:].unsqueeze(1).to_broadcast([P, HN, OC]), scalar=-0.25, in1=z[:],
+                    op0=ALU.mult, op1=ALU.add,
+                )
+            c2 = epool.tile([P, HN, OC], F32, name="c2")
+            nc.scalar.activation(out=c2[:], in_=c[:], func=ACT.Square)
+            if USE_TACC:
+                mB = sum_over_experts(c2, "mB")
+                rT = spool.tile([P, OC], F32, name="rT")
+                nc.scalar.activation(out=rT[:], in_=mB[:, 0:256], func=ACT.Abs_reciprocal_sqrt, scale=0.25)
+                r = back(mB, rT)
+            else:
+                q2 = spool.tile([P, 2, OC], F32, name="q2")
+                nc.vector.tensor_tensor(out=q2[:], in0=c2[:, 0:2, :], in1=c2[:, 2:4, :], op=ALU.add)
+                q4 = spool.tile([P, OC], F32, name="q4")
+                nc.vector.tensor_tensor(out=q4[:], in0=q2[:, 0, :], in1=q2[:, 1, :], op=ALU.add)
+                rs = spool.tile([P, OC], F32, name="rs")
+                nc.scalar.activation(out=rs[:], in_=q4[:], func=ACT.Abs_reciprocal_sqrt, scale=0.25)
+                r = rs[:]
+            u = upool.tile([P, HN, OC], F32, name="u")
+            for n in range(HN):
+                nc.vector.scalar_tensor_tensor(
+                    out=u[:, n, :], in0=r, scalar=1.0e8, in1=c[:, n, :], op0=ALU.min, op1=ALU.mult,
+                    accum_out=su[:, t, n : n + 1],
+                )
+            junk = spool.tile([P, OC], F32, name="junk")
+            for n in range(HN):
+                nc.scalar.activation(out=junk[:], in_=u[:, n, :], func=ACT.Square, accum_out=sq[:, t, n : n + 1])
+            utiles[t] = u
+
+        def finish(gi):
+            t0 = gi * GROUP
+            ts = slice(t0, t0 + GROUP)
+            mu = spool.tile([P, GROUP, HN], F32, name="mu")
+            nc.vector.tensor_scalar_mul(out=mu[:], in0=su[:, ts, :], scalar1=1.0 / OC)
+            m2 = spool.tile([P, GROUP, HN], F32, name="m2")
+            nc.vector.tensor_tensor(out=m2[:], in0=mu[:], in1=mu[:], op=ALU.mult)
+            var = spool.tile([P, GROUP, HN], F32, name="var")
+            nc.vector.scalar_tensor_tensor(
+                out=var[:], in0=sq[:, ts, :], scalar=1.0 / OC, in1=m2[:], op0=ALU.mult, op1=ALU.subtract
+            )
+            a = spool.tile([P, GROUP, HN], F32, name="a")
+            nc.scalar.activation(out=a[:], in_=var[:], func=ACT.Abs_reciprocal_sqrt)
+            a4 = spool.tile([P, GROUP, HN], F32, name="a4")
+            nc.vector.tensor_scalar(out=a4[:], in0=a[:], scalar1=1.0e8, scalar2=0.25, op0=ALU.min, op1=ALU.mult)
+            am = spool.tile([P, GROUP, HN], F32, name="am")
+            nc.vector.scalar_tensor_tensor(out=am[:], in0=mu[:], scalar=-1.0, in1=a4[:], op0=ALU.mult, op1=ALU.mult)
+            nk = spool.tile([P, GROUP], F32, name="nk")
+            nc.vector.tensor_reduce(out=nk[:], in_=am[:], axis=AX.X, op=ALU.add)
+            dl = spool.tile([P, GROUP, 3], F32, name="dl")
+            nc.vector.tensor_tensor(
+                out=dl[:], in0=a4[:, :, 0:3], in1=a4[:, :, 3:4].to_broadcast([P, GROUP, 3]), op=ALU.subtract
+            )
+            ob = opool.tile([P, GROUP, OC], F32, name="ob")
+            for k in range(GROUP):
+                u = utiles.pop(t0 + k)
+                f0 = spool.tile([P, OC], F32, name="f0")
+                nc.scalar.activation(
+                    out=f0[:], in_=u[:, 0, :], func=ACT.Identity, scale=dl[:, k, 0:1], bias=nk[:, k : k + 1]
+                )
+                f1 = spool.tile([P, OC], F32, name="f1")
+                nc.vector.scalar_tensor_tensor(
+                    out=f1[:], in0=u[:, 1, :], scalar=dl[:, k, 1:2], in1=f0[:], op0=ALU.mult, op1=ALU.add
+                )
+                nc.vector.scalar_tensor_tensor(
+                    out=ob[:, k, :], in0=u[:, 2, :], scalar=dl[:, k, 2:3], in1=f1[:], op0=ALU.mult, op1=ALU.add
+                )
+            nc.sync.dma_start(out=out_view[:, ts, :], in_=ob[:])
+
+        for i in range(NT + LAG):
+            if i + 3 < NT:
+                load(i + 3)
+            if i < NT:
+                main(i)
+            j = i - LAG
+            if j >= 0:
+                epi(j)
+                if j % GROUP == GROUP - 1:
+                    finish(j // GROUP)

@@ -15,31 +15,28 @@ AX = mybir.AxisListType
 P = 128
 B, HN, HM, OC = 4096, 4, 1024, 256
 NT = B // P
+NS = NT * HN
 GROUP = 4
+NG = NT // GROUP
 FLOPS = 2 * B * HN * HM * OC
 
-USE_TACC = True
-LAG = 1
+PIN = True
+AHEAD = 3
 
 
 def l_on_vector(t, n):
-    return n == 3 and t % 2 == 1
+    return n == 3 and t % 4 != 3
 
 
 def tile_tensormoe_pb_t_kernel(tc, h_pre, W_mo, weights_n, leak_n, out):
     nc = tc.nc
     with ExitStack() as ctx:
+        if PIN:
+            ctx.enter_context(tc.manual_schedule())
         const = ctx.enter_context(tc.tile_pool(name="const", bufs=1))
-        hpool = ctx.enter_context(tc.tile_pool(name="hpool", bufs=4))
-        lpool = ctx.enter_context(tc.tile_pool(name="lpool", bufs=4))
-        gpool = ctx.enter_context(tc.tile_pool(name="gpool", bufs=2))
-        qpool = ctx.enter_context(tc.tile_pool(name="qpool", bufs=2))
-        epool = ctx.enter_context(tc.tile_pool(name="epool", bufs=2))
-        upool = ctx.enter_context(tc.tile_pool(name="upool", bufs=2 * GROUP))
-        spool = ctx.enter_context(tc.tile_pool(name="spool", bufs=2))
-        opool = ctx.enter_context(tc.tile_pool(name="opool", bufs=2))
-        xpsum = ctx.enter_context(tc.psum_pool(name="xpsum", bufs=3))
-        ypsum = ctx.enter_context(tc.psum_pool(name="ypsum", bufs=3))
+        work = ctx.enter_context(tc.tile_pool(name="work", bufs=2))
+        xpsum = ctx.enter_context(tc.psum_pool(name="xpsum", bufs=4))
+        ypsum = ctx.enter_context(tc.psum_pool(name="ypsum", bufs=2))
         mpsum = ctx.enter_context(tc.psum_pool(name="mpsum", bufs=1))
 
         h_view = h_pre.rearrange("(p t) n m -> p t (n m)", t=NT)
@@ -50,12 +47,25 @@ def tile_tensormoe_pb_t_kernel(tc, h_pre, W_mo, weights_n, leak_n, out):
         wtb = const.tile([P, NT * HN], BF16)
         nc.sync.dma_start(out=wtb[:], in_=weights_n.rearrange("(p t) n -> p (t n)", t=NT))
 
-        htiles = {}
+        H = {}
+        X = {}
+        L = {}
+        G = {}
+        Q = {}
+        Y = {}
+        Z = {}
+        C = {}
+        C2 = {}
+        MA = {}
+        MB = {}
+        TT = {}
+        U = {}
+        FIN = {}
 
         def load(t):
-            hsb = hpool.tile([P, HN * HM], BF16, name="hsb")
+            hsb = work.tile([P, HN * HM], BF16, name="hsb", bufs=AHEAD + 2)
             nc.sync.dma_start(out=hsb[:], in_=h_view[:, t, :])
-            htiles[t] = hsb
+            H[t] = hsb
 
         load(0)
         wraw = const.tile([P, 16 * 512], BF16)
@@ -63,8 +73,8 @@ def tile_tensormoe_pb_t_kernel(tc, h_pre, W_mo, weights_n, leak_n, out):
             out=wraw[:].rearrange("p (a r) -> p a r", a=16),
             in_=W_mo.rearrange("n (g u p e) o -> p (n g u) (e o)", g=2, u=2, p=P, e=2),
         )
-        load(1)
-        load(2)
+        for t in range(1, AHEAD):
+            load(t)
 
         ident = const.tile([P, P], F32)
         make_identity(nc, ident[:])
@@ -81,74 +91,99 @@ def tile_tensormoe_pb_t_kernel(tc, h_pre, W_mo, weights_n, leak_n, out):
             in1=sg[:].unsqueeze(1).to_broadcast([P, NT, HN]),
             op=ALU.mult,
         )
-
         wgrp = const.tile([P, 8192], BF16, align_bytes=64)
-        wsrc = wraw[:].rearrange("p (a t o) -> p a o t", a=8, t=4, o=OC)
-        wdst = wgrp[:].rearrange("p (a o t) -> p a o t", a=8, t=4, o=OC)
-        nc.vector.tensor_copy(out=wdst[:, 0:4], in_=wsrc[:, 0:4])
-        nc.scalar.copy(out=wdst[:, 4:8], in_=wsrc[:, 4:8])
         wcodes = const.tile([P, 2048], U32, align_bytes=64)
         wscales = const.tile([P, 2048], U8, align_bytes=64)
-        for hf in range(2):
-            nc.vector.quantize_mx(
-                out=wcodes[:, hf * 1024 : (hf + 1) * 1024].bitcast(FP8X4),
-                scales=wscales[:, hf * 1024 : (hf + 1) * 1024],
-                in_=wgrp[:, hf * 4096 : (hf + 1) * 4096],
-            )
-
         su = const.tile([P, NT, HN], F32)
         sq = const.tile([P, NT, HN], F32)
 
-        ytiles = {}
-        utiles = {}
-
-        def main(t):
-            hsb = htiles.pop(t)
-            for n in range(HN):
-                sl = hsb[:, n * HM : (n + 1) * HM]
-                nc.vector.tensor_scalar(out=sl, in0=sl, scalar1=sg[:, n : n + 1], scalar2=None, op0=ALU.mult)
-            hw = hsb[:].bitcast(F32)
-            grp = gpool.tile([P, HN * HM], BF16, name="grp", align_bytes=64)
-            for n in range(HN):
-                xt = xpsum.tile([P, 512], F32, name="xt")
-                for u in range(2):
-                    for g in range(2):
-                        j = u * 2 + g
-                        c0 = n * 512 + g * 256 + u * 128
-                        nc.tensor.transpose(xt[:, j * P : (j + 1) * P], hw[:, c0 : c0 + P], ident[:])
-                xb = xt[:].bitcast(BF16)
-                lt = lpool.tile([P, HM], BF16, name="lt")
-                if l_on_vector(t, n):
-                    nc.vector.tensor_scalar(out=lt[:], in0=xb, scalar1=lk[:, n : n + 1], scalar2=None, op0=ALU.mult)
-                else:
-                    nc.scalar.activation(out=lt[:], in_=xb, func=ACT.Copy, scale=lk[:, n : n + 1])
-                nc.vector.tensor_tensor(
-                    out=grp[:, n * HM : (n + 1) * HM].rearrange("p (w u e) -> p w u e", u=2, e=2),
-                    in0=lt[:].rearrange("p (u w e) -> p w u e", u=2, e=2),
-                    in1=xb.rearrange("p (u w e) -> p w u e", u=2, e=2),
-                    op=ALU.max,
+        def prep_w():
+            wsrc = wraw[:].rearrange("p (a t o) -> p a o t", a=8, t=4, o=OC)
+            wdst = wgrp[:].rearrange("p (a o t) -> p a o t", a=8, t=4, o=OC)
+            nc.scalar.copy(out=wdst[:, 5:8], in_=wsrc[:, 5:8])
+            nc.vector.tensor_copy(out=wdst[:, 0:5], in_=wsrc[:, 0:5])
+            for hf in range(2):
+                nc.vector.quantize_mx(
+                    out=wcodes[:, hf * 1024 : (hf + 1) * 1024].bitcast(FP8X4),
+                    scales=wscales[:, hf * 1024 : (hf + 1) * 1024],
+                    in_=wgrp[:, hf * 4096 : (hf + 1) * 4096],
                 )
-            codes = qpool.tile([P, HN * 256], U32, name="codes", align_bytes=64)
-            scales = qpool.tile([P, HN * 256], U8, name="scales", align_bytes=64)
+
+        def flip(s):
+            t, n = divmod(s, HN)
+            sl = H[t][:, n * HM : (n + 1) * HM]
+            nc.vector.tensor_scalar(out=sl, in0=sl, scalar1=sg[:, n : n + 1], scalar2=None, op0=ALU.mult)
+
+        def transposes(s):
+            t, n = divmod(s, HN)
+            hw = H[t][:].bitcast(F32)
+            xt = xpsum.tile([P, 512], F32, name="xt")
+            for u in range(2):
+                for g in range(2):
+                    j = u * 2 + g
+                    c0 = n * 512 + g * 256 + u * 128
+                    nc.tensor.transpose(xt[:, j * P : (j + 1) * P], hw[:, c0 : c0 + P], ident[:])
+            X[s] = xt
+            if n == HN - 1:
+                H.pop(t)
+
+        def leak_times(s):
+            t, n = divmod(s, HN)
+            xb = X[s][:].bitcast(BF16)
+            lt = work.tile([P, HM], BF16, name="lt", bufs=3)
+            if l_on_vector(t, n):
+                nc.vector.tensor_scalar(out=lt[:], in0=xb, scalar1=lk[:, n : n + 1], scalar2=None, op0=ALU.mult)
+            else:
+                nc.scalar.activation(out=lt[:], in_=xb, func=ACT.Copy, scale=lk[:, n : n + 1])
+            L[s] = lt
+
+        def take_max(s):
+            xb = X.pop(s)[:].bitcast(BF16)
+            lt = L.pop(s)
+            grp = work.tile([P, HM], BF16, name="grp", bufs=3, align_bytes=64)
+            nc.vector.tensor_tensor(
+                out=grp[:].rearrange("p (w u e) -> p w u e", u=2, e=2),
+                in0=lt[:].rearrange("p (u w e) -> p w u e", u=2, e=2),
+                in1=xb.rearrange("p (u w e) -> p w u e", u=2, e=2),
+                op=ALU.max,
+            )
+            G[s] = grp
+
+        def quantise(s):
+            grp = G.pop(s)
+            codes = work.tile([P, 256], U32, name="codes", bufs=3, align_bytes=64)
+            scales = work.tile([P, 256], U8, name="scales", bufs=3, align_bytes=64)
             nc.vector.quantize_mx(out=codes[:].bitcast(FP8X4), scales=scales[:], in_=grp[:])
-            ys = []
-            for pr in range(2):
+            Q[s] = (codes, scales)
+
+        def mx(s):
+            t, n = divmod(s, HN)
+            codes, scales = Q.pop(s)
+            if n % 2 == 0:
                 y = ypsum.tile([P, 2, OC], F32, name="y")
-                for nn in range(2):
-                    n = pr * 2 + nn
-                    for g in range(2):
-                        a = n * 2 + g
-                        nc.tensor.matmul_mx(
-                            out=y[:, nn, :],
-                            lhsT=codes[:, a * P : (a + 1) * P].bitcast(FP8X4),
-                            lhsT_scale=scales[:, a * P : (a + 1) * P],
-                            rhs=wcodes[:, a * OC : (a + 1) * OC].bitcast(FP8X4),
-                            rhs_scale=wscales[:, a * OC : (a + 1) * OC],
-                            start=(g == 0),
-                            stop=(g == 1),
-                        )
-                ys.append(y)
-            ytiles[t] = ys
+                Y[s // 2] = y
+            y = Y[s // 2]
+            for g in range(2):
+                a = n * 2 + g
+                nc.tensor.matmul_mx(
+                    out=y[:, n % 2, :],
+                    lhsT=codes[:, g * P : (g + 1) * P].bitcast(FP8X4),
+                    lhsT_scale=scales[:, g * P : (g + 1) * P],
+                    rhs=wcodes[:, a * OC : (a + 1) * OC].bitcast(FP8X4),
+                    rhs_scale=wscales[:, a * OC : (a + 1) * OC],
+                    start=(g == 0),
+                    stop=(g == 1),
+                )
+
+        def weigh(s):
+            t, n = divmod(s, HN)
+            if n == 0:
+                z = work.tile([P, HN, OC], F32, name="z", bufs=3)
+                Z[t] = z
+            y = Y[s // 2]
+            nc.scalar.activation(out=Z[t][:, n, :], in_=y[:, n % 2, :], func=ACT.Copy, scale=wp[:, t, n : n + 1])
+            if n % 2 == 1:
+                Y.pop(s // 2)
 
         def sum_over_experts(src, tagname):
             m = mpsum.tile([P, 512], F32, name=tagname)
@@ -164,104 +199,186 @@ def tile_tensormoe_pb_t_kernel(tc, h_pre, W_mo, weights_n, leak_n, out):
                     )
             return m
 
-        def back(m, srcT):
+        def back(m, src_t):
             for hf in range(2):
-                nc.tensor.transpose(m[:, 256 + hf * P : 256 + (hf + 1) * P], srcT[:, hf * P : (hf + 1) * P], ident[:])
-            return m[:, 256:512]
+                nc.tensor.transpose(m[:, 256 + hf * P : 256 + (hf + 1) * P], src_t[:, hf * P : (hf + 1) * P], ident[:])
 
-        def epi(t):
-            ys = ytiles.pop(t)
-            z = epool.tile([P, HN, OC], F32, name="z")
-            for n in range(HN):
-                nc.scalar.activation(out=z[:, n, :], in_=ys[n // 2][:, n % 2, :], func=ACT.Copy, scale=wp[:, t, n : n + 1])
-            c = epool.tile([P, HN, OC], F32, name="c")
-            if USE_TACC:
-                mA = sum_over_experts(z, "mA")
-                nmT = spool.tile([P, OC], F32, name="nmT")
-                nc.scalar.activation(out=nmT[:], in_=mA[:, 0:256], func=ACT.Copy, scale=-0.25)
-                nm = back(mA, nmT)
-                nc.vector.tensor_tensor(out=c[:], in0=z[:], in1=nm.unsqueeze(1).to_broadcast([P, HN, OC]), op=ALU.add)
-            else:
-                s2 = spool.tile([P, 2, OC], F32, name="s2")
-                nc.vector.tensor_tensor(out=s2[:], in0=z[:, 0:2, :], in1=z[:, 2:4, :], op=ALU.add)
-                s4 = spool.tile([P, OC], F32, name="s4")
-                nc.vector.tensor_tensor(out=s4[:], in0=s2[:, 0, :], in1=s2[:, 1, :], op=ALU.add)
-                nc.vector.scalar_tensor_tensor(
-                    out=c[:], in0=s4[:].unsqueeze(1).to_broadcast([P, HN, OC]), scalar=-0.25, in1=z[:],
-                    op0=ALU.mult, op1=ALU.add,
-                )
-            c2 = epool.tile([P, HN, OC], F32, name="c2")
-            nc.scalar.activation(out=c2[:], in_=c[:], func=ACT.Square)
-            if USE_TACC:
-                mB = sum_over_experts(c2, "mB")
-                rT = spool.tile([P, OC], F32, name="rT")
-                nc.scalar.activation(out=rT[:], in_=mB[:, 0:256], func=ACT.Abs_reciprocal_sqrt, scale=0.25)
-                r = back(mB, rT)
-            else:
-                q2 = spool.tile([P, 2, OC], F32, name="q2")
-                nc.vector.tensor_tensor(out=q2[:], in0=c2[:, 0:2, :], in1=c2[:, 2:4, :], op=ALU.add)
-                q4 = spool.tile([P, OC], F32, name="q4")
-                nc.vector.tensor_tensor(out=q4[:], in0=q2[:, 0, :], in1=q2[:, 1, :], op=ALU.add)
-                rs = spool.tile([P, OC], F32, name="rs")
-                nc.scalar.activation(out=rs[:], in_=q4[:], func=ACT.Abs_reciprocal_sqrt, scale=0.25)
-                r = rs[:]
-            u = upool.tile([P, HN, OC], F32, name="u")
+        def e_sum(t):
+            MA[t] = sum_over_experts(Z[t], "mA")
+
+        def e_nm(t):
+            nmt = work.tile([P, OC], F32, name="nmt")
+            nc.scalar.activation(out=nmt[:], in_=MA[t][:, 0:256], func=ACT.Copy, scale=-0.25)
+            TT[t] = nmt
+
+        def e_nmback(t):
+            back(MA[t], TT.pop(t))
+
+        def e_centre(t):
+            c = work.tile([P, HN, OC], F32, name="c", bufs=3)
+            nm = MA.pop(t)[:, 256:512]
+            nc.vector.tensor_tensor(
+                out=c[:], in0=Z.pop(t)[:], in1=nm.unsqueeze(1).to_broadcast([P, HN, OC]), op=ALU.add
+            )
+            C[t] = c
+
+        def e_square(t):
+            c2 = work.tile([P, HN, OC], F32, name="c2")
+            nc.scalar.activation(out=c2[:], in_=C[t][:], func=ACT.Square)
+            C2[t] = c2
+
+        def e_q(t):
+            MB[t] = sum_over_experts(C2.pop(t), "mB")
+
+        def e_r(t):
+            rt = work.tile([P, OC], F32, name="rt")
+            nc.scalar.activation(out=rt[:], in_=MB[t][:, 0:256], func=ACT.Abs_reciprocal_sqrt, scale=0.25)
+            TT[t] = rt
+
+        def e_rback(t):
+            back(MB[t], TT.pop(t))
+
+        def e_u(t):
+            u = work.tile([P, HN, OC], F32, name="u", bufs=9)
+            r = MB.pop(t)[:, 256:512]
+            c = C.pop(t)
             for n in range(HN):
                 nc.vector.scalar_tensor_tensor(
                     out=u[:, n, :], in0=r, scalar=1.0e8, in1=c[:, n, :], op0=ALU.min, op1=ALU.mult,
                     accum_out=su[:, t, n : n + 1],
                 )
-            junk = spool.tile([P, OC], F32, name="junk")
-            for n in range(HN):
-                nc.scalar.activation(out=junk[:], in_=u[:, n, :], func=ACT.Square, accum_out=sq[:, t, n : n + 1])
-            utiles[t] = u
+            U[t] = u
 
-        def finish(gi):
+        def e_usq(t, n):
+            junk = work.tile([P, OC], F32, name="junk")
+            nc.scalar.activation(out=junk[:], in_=U[t][:, n, :], func=ACT.Square, accum_out=sq[:, t, n : n + 1])
+
+        def small(name):
+            return work.tile([P, GROUP, HN], F32, name=name)
+
+        def fin(gi, step):
             t0 = gi * GROUP
             ts = slice(t0, t0 + GROUP)
-            mu = spool.tile([P, GROUP, HN], F32, name="mu")
-            nc.vector.tensor_scalar_mul(out=mu[:], in0=su[:, ts, :], scalar1=1.0 / OC)
-            m2 = spool.tile([P, GROUP, HN], F32, name="m2")
-            nc.vector.tensor_tensor(out=m2[:], in0=mu[:], in1=mu[:], op=ALU.mult)
-            var = spool.tile([P, GROUP, HN], F32, name="var")
-            nc.vector.scalar_tensor_tensor(
-                out=var[:], in0=sq[:, ts, :], scalar=1.0 / OC, in1=m2[:], op0=ALU.mult, op1=ALU.subtract
-            )
-            a = spool.tile([P, GROUP, HN], F32, name="a")
-            nc.scalar.activation(out=a[:], in_=var[:], func=ACT.Abs_reciprocal_sqrt)
-            a4 = spool.tile([P, GROUP, HN], F32, name="a4")
-            nc.vector.tensor_scalar(out=a4[:], in0=a[:], scalar1=1.0e8, scalar2=0.25, op0=ALU.min, op1=ALU.mult)
-            am = spool.tile([P, GROUP, HN], F32, name="am")
-            nc.vector.scalar_tensor_tensor(out=am[:], in0=mu[:], scalar=-1.0, in1=a4[:], op0=ALU.mult, op1=ALU.mult)
-            nk = spool.tile([P, GROUP], F32, name="nk")
-            nc.vector.tensor_reduce(out=nk[:], in_=am[:], axis=AX.X, op=ALU.add)
-            dl = spool.tile([P, GROUP, 3], F32, name="dl")
-            nc.vector.tensor_tensor(
-                out=dl[:], in0=a4[:, :, 0:3], in1=a4[:, :, 3:4].to_broadcast([P, GROUP, 3]), op=ALU.subtract
-            )
-            ob = opool.tile([P, GROUP, OC], F32, name="ob")
-            for k in range(GROUP):
-                u = utiles.pop(t0 + k)
-                f0 = spool.tile([P, OC], F32, name="f0")
-                nc.scalar.activation(
-                    out=f0[:], in_=u[:, 0, :], func=ACT.Identity, scale=dl[:, k, 0:1], bias=nk[:, k : k + 1]
-                )
-                f1 = spool.tile([P, OC], F32, name="f1")
+            if step == 0:
+                mu = small("mu")
+                nc.vector.tensor_scalar_mul(out=mu[:], in0=su[:, ts, :], scalar1=1.0 / OC)
+                FIN[gi] = {"mu": mu}
+            f = FIN[gi]
+            if step == 1:
+                m2 = small("m2")
+                nc.vector.tensor_tensor(out=m2[:], in0=f["mu"][:], in1=f["mu"][:], op=ALU.mult)
+                f["m2"] = m2
+            if step == 2:
+                var = small("var")
                 nc.vector.scalar_tensor_tensor(
-                    out=f1[:], in0=u[:, 1, :], scalar=dl[:, k, 1:2], in1=f0[:], op0=ALU.mult, op1=ALU.add
+                    out=var[:], in0=sq[:, ts, :], scalar=1.0 / OC, in1=f["m2"][:], op0=ALU.mult, op1=ALU.subtract
                 )
+                f["var"] = var
+            if step == 3:
+                a = small("a")
+                nc.scalar.activation(out=a[:], in_=f["var"][:], func=ACT.Abs_reciprocal_sqrt)
+                f["a"] = a
+            if step == 4:
+                a4 = small("a4")
+                nc.vector.tensor_scalar(out=a4[:], in0=f["a"][:], scalar1=1.0e8, scalar2=0.25, op0=ALU.min, op1=ALU.mult)
+                f["a4"] = a4
+            if step == 5:
+                am = small("am")
                 nc.vector.scalar_tensor_tensor(
-                    out=ob[:, k, :], in0=u[:, 2, :], scalar=dl[:, k, 2:3], in1=f1[:], op0=ALU.mult, op1=ALU.add
+                    out=am[:], in0=f["mu"][:], scalar=-1.0, in1=f["a4"][:], op0=ALU.mult, op1=ALU.mult
                 )
-            nc.sync.dma_start(out=out_view[:, ts, :], in_=ob[:])
+                f["am"] = am
+                dl = work.tile([P, GROUP, 3], F32, name="dl")
+                nc.vector.tensor_tensor(
+                    out=dl[:], in0=f["a4"][:, :, 0:3], in1=f["a4"][:, :, 3:4].to_broadcast([P, GROUP, 3]), op=ALU.subtract
+                )
+                f["dl"] = dl
+            if step == 6:
+                nk = work.tile([P, GROUP], F32, name="nk")
+                nc.vector.tensor_reduce(out=nk[:], in_=f["am"][:], axis=AX.X, op=ALU.add)
+                f["nk"] = nk
+                ob = work.tile([P, GROUP, OC], F32, name="ob")
+                f["ob"] = ob
 
-        for i in range(NT + LAG):
-            if i + 3 < NT:
-                load(i + 3)
-            if i < NT:
-                main(i)
-            j = i - LAG
-            if j >= 0:
-                epi(j)
-                if j % GROUP == GROUP - 1:
-                    finish(j // GROUP)
+        def fin_first(gi, k):
+            f = FIN[gi]
+            f0 = work.tile([P, OC], F32, name="f0")
+            nc.scalar.activation(
+                out=f0[:], in_=U[gi * GROUP + k][:, 0, :], func=ACT.Identity,
+                scale=f["dl"][:, k, 0:1], bias=f["nk"][:, k : k + 1],
+            )
+            f[("f0", k)] = f0
+
+        def fin_rest(gi, k):
+            f = FIN[gi]
+            u = U.pop(gi * GROUP + k)
+            f1 = work.tile([P, OC], F32, name="f1")
+            nc.vector.scalar_tensor_tensor(
+                out=f1[:], in0=u[:, 1, :], scalar=f["dl"][:, k, 1:2], in1=f[("f0", k)][:], op0=ALU.mult, op1=ALU.add
+            )
+            nc.vector.scalar_tensor_tensor(
+                out=f["ob"][:, k, :], in0=u[:, 2, :], scalar=f["dl"][:, k, 2:3], in1=f1[:], op0=ALU.mult, op1=ALU.add
+            )
+
+        def fin_store(gi):
+            f = FIN.pop(gi)
+            nc.sync.dma_start(out=out_view[:, gi * GROUP : (gi + 1) * GROUP, :], in_=f["ob"][:])
+
+        def bank(x):
+            return 0 <= x < NS
+
+        def tile_at(x):
+            return x % HN == 0 and 0 <= x // HN < NT
+
+        last = 16 * (NG - 1) + 35 + 13
+        for tau in range(last + 1):
+            if tau % HN == 0 and tau // HN + AHEAD < NT:
+                load(tau // HN + AHEAD)
+            if bank(tau - 5):
+                mx(tau - 5)
+            if tile_at(tau - 10):
+                e_sum((tau - 10) // HN)
+            if tile_at(tau - 12):
+                e_nmback((tau - 12) // HN)
+            if tile_at(tau - 15):
+                e_q((tau - 15) // HN)
+            if tile_at(tau - 17):
+                e_rback((tau - 17) // HN)
+            if bank(tau - 1):
+                transposes(tau - 1)
+            if tile_at(tau - 11):
+                e_nm((tau - 11) // HN)
+            if tile_at(tau - 16):
+                e_r((tau - 16) // HN)
+            if bank(tau - 6):
+                weigh(tau - 6)
+            if bank(tau - 2):
+                leak_times(tau - 2)
+            if tile_at(tau - 14):
+                e_square((tau - 14) // HN)
+            for n in range(HN):
+                if tile_at(tau - 19 - n):
+                    e_usq((tau - 19 - n) // HN, n)
+            if bank(tau - 4):
+                quantise(tau - 4)
+            if bank(tau):
+                flip(tau)
+            if tau == 0:
+                prep_w()
+            if bank(tau - 3):
+                take_max(tau - 3)
+            if tile_at(tau - 13):
+                e_centre((tau - 13) // HN)
+            if tile_at(tau - 18):
+                e_u((tau - 18) // HN)
+            x = tau - 35
+            if x >= 0:
+                gi, step = divmod(x, 16)
+                if gi < NG and step <= 6:
+                    fin(gi, step)
+                if gi < NG and 7 <= step <= 10:
+                    fin_first(gi, step - 7)
+                if gi < NG and 8 <= step <= 11:
+                    fin_rest(gi, step - 8)
+                if gi < NG and step == 13:
+                    fin_store(gi)

@@ -15,28 +15,31 @@ AX = mybir.AxisListType
 P = 128
 B, HN, HM, OC = 4096, 4, 1024, 256
 NT = B // P
-NS = NT * HN
 GROUP = 4
-NG = NT // GROUP
 FLOPS = 2 * B * HN * HM * OC
 
-PIN = True
-AHEAD = 3
+USE_TACC = True
+LAG = 1
 
 
 def l_on_vector(t, n):
-    return n == 3 and t % 4 != 3
+    return n == 3 and t % 2 == 1
 
 
 def tile_tensormoe_pb_t_kernel(tc, h_pre, W_mo, weights_n, leak_n, out):
     nc = tc.nc
     with ExitStack() as ctx:
-        if PIN:
-            ctx.enter_context(tc.manual_schedule())
         const = ctx.enter_context(tc.tile_pool(name="const", bufs=1))
-        work = ctx.enter_context(tc.tile_pool(name="work", bufs=2))
-        xpsum = ctx.enter_context(tc.psum_pool(name="xpsum", bufs=4))
-        ypsum = ctx.enter_context(tc.psum_pool(name="ypsum", bufs=2))
+        hpool = ctx.enter_context(tc.tile_pool(name="hpool", bufs=4))
+        lpool = ctx.enter_context(tc.tile_pool(name="lpool", bufs=4))
+        gpool = ctx.enter_context(tc.tile_pool(name="gpool", bufs=2))
+        qpool = ctx.enter_context(tc.tile_pool(name="qpool", bufs=2))
+        epool = ctx.enter_context(tc.tile_pool(name="epool", bufs=2))
+        upool = ctx.enter_context(tc.tile_pool(name="upool", bufs=2 * GROUP))
+        spool = ctx.enter_context(tc.tile_pool(name="spool", bufs=2))
+        opool = ctx.enter_context(tc.tile_pool(name="opool", bufs=2))
+        xpsum = ctx.enter_context(tc.psum_pool(name="xpsum", bufs=3))
+        ypsum = ctx.enter_context(tc.psum_pool(name="ypsum", bufs=3))
         mpsum = ctx.enter_context(tc.psum_pool(name="mpsum", bufs=1))
 
         h_view = h_pre.rearrange("(p t) n m -> p t (n m)", t=NT)
@@ -47,25 +50,12 @@ def tile_tensormoe_pb_t_kernel(tc, h_pre, W_mo, weights_n, leak_n, out):
         wtb = const.tile([P, NT * HN], BF16)
         nc.sync.dma_start(out=wtb[:], in_=weights_n.rearrange("(p t) n -> p (t n)", t=NT))
 
-        H = {}
-        X = {}
-        L = {}
-        G = {}
-        Q = {}
-        Y = {}
-        Z = {}
-        C = {}
-        C2 = {}
-        MA = {}
-        MB = {}
-        TT = {}
-        U = {}
-        FIN = {}
+        htiles = {}
 
         def load(t):
-            hsb = work.tile([P, HN * HM], BF16, name="hsb", bufs=AHEAD + 2)
+            hsb = hpool.tile([P, HN * HM], BF16, name="hsb")
             nc.sync.dma_start(out=hsb[:], in_=h_view[:, t, :])
-            H[t] = hsb
+            htiles[t] = hsb
 
         load(0)
         wraw = const.tile([P, 16 * 512], BF16)
@@ -73,8 +63,8 @@ def tile_tensormoe_pb_t_kernel(tc, h_pre, W_mo, weights_n, leak_n, out):
             out=wraw[:].rearrange("p (a r) -> p a r", a=16),
             in_=W_mo.rearrange("n (g u p e) o -> p (n g u) (e o)", g=2, u=2, p=P, e=2),
         )
-        for t in range(1, AHEAD):
-            load(t)
+        load(1)
+        load(2)
 
         ident = const.tile([P, P], F32)
         make_identity(nc, ident[:])
@@ -91,99 +81,73 @@ def tile_tensormoe_pb_t_kernel(tc, h_pre, W_mo, weights_n, leak_n, out):
             in1=sg[:].unsqueeze(1).to_broadcast([P, NT, HN]),
             op=ALU.mult,
         )
+
         wgrp = const.tile([P, 8192], BF16, align_bytes=64)
-        wcodes = const.tile([P, 2048], U32, align_bytes=64)
-        wscales = const.tile([P, 2048], U8, align_bytes=64)
+        wsrc = wraw[:].rearrange("p (a t o) -> p a o t", a=8, t=4, o=OC)
+        wdst = wgrp[:].rearrange("p (a o t) -> p a o t", a=8, t=4, o=OC)
+        nc.vector.tensor_copy(out=wdst[:, 0:4], in_=wsrc[:, 0:4])
+        nc.scalar.copy(out=wdst[:, 4:8], in_=wsrc[:, 4:8])
+        wcodes = const.tile([P, 2304], U32, align_bytes=64)
+        wscales = const.tile([P, 2304], U8, align_bytes=64)
+        nc.vector.quantize_mx(out=wcodes[:, 2048:2304].bitcast(FP8X4), scales=wscales[:, 2048:2304], in_=wgrp[:, 0:1024])
+        for hf in range(2):
+            nc.vector.quantize_mx(
+                out=wcodes[:, hf * 1024 : (hf + 1) * 1024].bitcast(FP8X4),
+                scales=wscales[:, hf * 1024 : (hf + 1) * 1024],
+                in_=wgrp[:, hf * 4096 : (hf + 1) * 4096],
+            )
+
         su = const.tile([P, NT, HN], F32)
         sq = const.tile([P, NT, HN], F32)
 
-        def prep_w():
-            wsrc = wraw[:].rearrange("p (a t o) -> p a o t", a=8, t=4, o=OC)
-            wdst = wgrp[:].rearrange("p (a o t) -> p a o t", a=8, t=4, o=OC)
-            nc.scalar.copy(out=wdst[:, 5:8], in_=wsrc[:, 5:8])
-            nc.vector.tensor_copy(out=wdst[:, 0:5], in_=wsrc[:, 0:5])
-            for hf in range(2):
-                nc.vector.quantize_mx(
-                    out=wcodes[:, hf * 1024 : (hf + 1) * 1024].bitcast(FP8X4),
-                    scales=wscales[:, hf * 1024 : (hf + 1) * 1024],
-                    in_=wgrp[:, hf * 4096 : (hf + 1) * 4096],
+        ytiles = {}
+        utiles = {}
+
+        def main(t):
+            hsb = htiles.pop(t)
+            for n in range(HN):
+                sl = hsb[:, n * HM : (n + 1) * HM]
+                nc.vector.tensor_scalar(out=sl, in0=sl, scalar1=sg[:, n : n + 1], scalar2=None, op0=ALU.mult)
+            hw = hsb[:].bitcast(F32)
+            grp = gpool.tile([P, HN * HM], BF16, name="grp", align_bytes=64)
+            for n in range(HN):
+                xt = xpsum.tile([P, 512], F32, name="xt")
+                for u in range(2):
+                    for g in range(2):
+                        j = u * 2 + g
+                        c0 = n * 512 + g * 256 + u * 128
+                        nc.tensor.transpose(xt[:, j * P : (j + 1) * P], hw[:, c0 : c0 + P], ident[:])
+                xb = xt[:].bitcast(BF16)
+                lt = lpool.tile([P, HM], BF16, name="lt")
+                if l_on_vector(t, n):
+                    nc.vector.tensor_scalar(out=lt[:], in0=xb, scalar1=lk[:, n : n + 1], scalar2=None, op0=ALU.mult)
+                else:
+                    nc.scalar.activation(out=lt[:], in_=xb, func=ACT.Copy, scale=lk[:, n : n + 1])
+                nc.vector.tensor_tensor(
+                    out=grp[:, n * HM : (n + 1) * HM].rearrange("p (w u e) -> p w u e", u=2, e=2),
+                    in0=lt[:].rearrange("p (u w e) -> p w u e", u=2, e=2),
+                    in1=xb.rearrange("p (u w e) -> p w u e", u=2, e=2),
+                    op=ALU.max,
                 )
-
-        def flip(s):
-            t, n = divmod(s, HN)
-            sl = H[t][:, n * HM : (n + 1) * HM]
-            nc.vector.tensor_scalar(out=sl, in0=sl, scalar1=sg[:, n : n + 1], scalar2=None, op0=ALU.mult)
-
-        def transposes(s):
-            t, n = divmod(s, HN)
-            hw = H[t][:].bitcast(F32)
-            xt = xpsum.tile([P, 512], F32, name="xt")
-            for u in range(2):
-                for g in range(2):
-                    j = u * 2 + g
-                    c0 = n * 512 + g * 256 + u * 128
-                    nc.tensor.transpose(xt[:, j * P : (j + 1) * P], hw[:, c0 : c0 + P], ident[:])
-            X[s] = xt
-            if n == HN - 1:
-                H.pop(t)
-
-        def leak_times(s):
-            t, n = divmod(s, HN)
-            xb = X[s][:].bitcast(BF16)
-            lt = work.tile([P, HM], BF16, name="lt", bufs=3)
-            if l_on_vector(t, n):
-                nc.vector.tensor_scalar(out=lt[:], in0=xb, scalar1=lk[:, n : n + 1], scalar2=None, op0=ALU.mult)
-            else:
-                nc.scalar.activation(out=lt[:], in_=xb, func=ACT.Copy, scale=lk[:, n : n + 1])
-            L[s] = lt
-
-        def take_max(s):
-            xb = X.pop(s)[:].bitcast(BF16)
-            lt = L.pop(s)
-            grp = work.tile([P, HM], BF16, name="grp", bufs=3, align_bytes=64)
-            nc.vector.tensor_tensor(
-                out=grp[:].rearrange("p (w u e) -> p w u e", u=2, e=2),
-                in0=lt[:].rearrange("p (u w e) -> p w u e", u=2, e=2),
-                in1=xb.rearrange("p (u w e) -> p w u e", u=2, e=2),
-                op=ALU.max,
-            )
-            G[s] = grp
-
-        def quantise(s):
-            grp = G.pop(s)
-            codes = work.tile([P, 256], U32, name="codes", bufs=3, align_bytes=64)
-            scales = work.tile([P, 256], U8, name="scales", bufs=3, align_bytes=64)
+            codes = qpool.tile([P, HN * 256], U32, name="codes", align_bytes=64)
+            scales = qpool.tile([P, HN * 256], U8, name="scales", align_bytes=64)
             nc.vector.quantize_mx(out=codes[:].bitcast(FP8X4), scales=scales[:], in_=grp[:])
-            Q[s] = (codes, scales)
-
-        def mx(s):
-            t, n = divmod(s, HN)
-            codes, scales = Q.pop(s)
-            if n % 2 == 0:
-                y = ypsum.tile([P, 2, OC], F32, name="y")
-                Y[s // 2] = y
-            y = Y[s // 2]
-            for g in range(2):
-                a = n * 2 + g
-                nc.tensor.matmul_mx(
-                    out=y[:, n % 2, :],
-                    lhsT=codes[:, g * P : (g + 1) * P].bitcast(FP8X4),
-                    lhsT_scale=scales[:, g * P : (g + 1) * P],
-                    rhs=wcodes[:, a * OC : (a + 1) * OC].bitcast(FP8X4),
-                    rhs_scale=wscales[:, a * OC : (a + 1) * OC],
-                    start=(g == 0),
-                    stop=(g == 1),
-                )
-
-        def weigh(s):
-            t, n = divmod(s, HN)
-            if n == 0:
-                z = work.tile([P, HN, OC], F32, name="z", bufs=3)
-                Z[t] = z
-            y = Y[s // 2]
-            nc.scalar.activation(out=Z[t][:, n, :], in_=y[:, n % 2, :], func=ACT.Copy, scale=wp[:, t, n : n + 1])
-            if n % 2 == 1:
-                Y.pop(s // 2)
+            ys = []
+            for n in range(HN):
+                y = ypsum.tile([P, 512], F32, name="y")
+                for g in range(2):
+                    a = n * 2 + g
+                    nc.tensor.matmul_mx(
+                        out=y[:],
+                        lhsT=codes[:, a * P : (a + 1) * P].bitcast(FP8X4),
+                        lhsT_scale=scales[:, a * P : (a + 1) * P],
+                        rhs=wcodes[:, a * OC : a * OC + 512].bitcast(FP8X4),
+                        rhs_scale=wscales[:, a * OC : a * OC + 512],
+                        start=(g == 0),
+                        stop=(g == 1),
+                    )
+                ys.append(y)
+            ytiles[t] = ys
 
         def sum_over_experts(src, tagname):
             m = mpsum.tile([P, 512], F32, name=tagname)
@@ -199,186 +163,104 @@ def tile_tensormoe_pb_t_kernel(tc, h_pre, W_mo, weights_n, leak_n, out):
                     )
             return m
 
-        def back(m, src_t):
+        def back(m, srcT):
             for hf in range(2):
-                nc.tensor.transpose(m[:, 256 + hf * P : 256 + (hf + 1) * P], src_t[:, hf * P : (hf + 1) * P], ident[:])
+                nc.tensor.transpose(m[:, 256 + hf * P : 256 + (hf + 1) * P], srcT[:, hf * P : (hf + 1) * P], ident[:])
+            return m[:, 256:512]
 
-        def e_sum(t):
-            MA[t] = sum_over_experts(Z[t], "mA")
-
-        def e_nm(t):
-            nmt = work.tile([P, OC], F32, name="nmt")
-            nc.scalar.activation(out=nmt[:], in_=MA[t][:, 0:256], func=ACT.Copy, scale=-0.25)
-            TT[t] = nmt
-
-        def e_nmback(t):
-            back(MA[t], TT.pop(t))
-
-        def e_centre(t):
-            c = work.tile([P, HN, OC], F32, name="c", bufs=3)
-            nm = MA.pop(t)[:, 256:512]
-            nc.vector.tensor_tensor(
-                out=c[:], in0=Z.pop(t)[:], in1=nm.unsqueeze(1).to_broadcast([P, HN, OC]), op=ALU.add
-            )
-            C[t] = c
-
-        def e_square(t):
-            c2 = work.tile([P, HN, OC], F32, name="c2")
-            nc.scalar.activation(out=c2[:], in_=C[t][:], func=ACT.Square)
-            C2[t] = c2
-
-        def e_q(t):
-            MB[t] = sum_over_experts(C2.pop(t), "mB")
-
-        def e_r(t):
-            rt = work.tile([P, OC], F32, name="rt")
-            nc.scalar.activation(out=rt[:], in_=MB[t][:, 0:256], func=ACT.Abs_reciprocal_sqrt, scale=0.25)
-            TT[t] = rt
-
-        def e_rback(t):
-            back(MB[t], TT.pop(t))
-
-        def e_u(t):
-            u = work.tile([P, HN, OC], F32, name="u", bufs=9)
-            r = MB.pop(t)[:, 256:512]
-            c = C.pop(t)
+        def epi(t):
+            ys = ytiles.pop(t)
+            z = epool.tile([P, HN, OC], F32, name="z")
+            for n in range(HN):
+                nc.scalar.activation(out=z[:, n, :], in_=ys[n][:, 0:OC], func=ACT.Copy, scale=wp[:, t, n : n + 1])
+            c = epool.tile([P, HN, OC], F32, name="c")
+            if USE_TACC:
+                mA = sum_over_experts(z, "mA")
+                nmT = spool.tile([P, OC], F32, name="nmT")
+                nc.scalar.activation(out=nmT[:], in_=mA[:, 0:256], func=ACT.Copy, scale=-0.25)
+                nm = back(mA, nmT)
+                nc.vector.tensor_tensor(out=c[:], in0=z[:], in1=nm.unsqueeze(1).to_broadcast([P, HN, OC]), op=ALU.add)
+            else:
+                s2 = spool.tile([P, 2, OC], F32, name="s2")
+                nc.vector.tensor_tensor(out=s2[:], in0=z[:, 0:2, :], in1=z[:, 2:4, :], op=ALU.add)
+                s4 = spool.tile([P, OC], F32, name="s4")
+                nc.vector.tensor_tensor(out=s4[:], in0=s2[:, 0, :], in1=s2[:, 1, :], op=ALU.add)
+                nc.vector.scalar_tensor_tensor(
+                    out=c[:], in0=s4[:].unsqueeze(1).to_broadcast([P, HN, OC]), scalar=-0.25, in1=z[:],
+                    op0=ALU.mult, op1=ALU.add,
+                )
+            c2 = epool.tile([P, HN, OC], F32, name="c2")
+            nc.scalar.activation(out=c2[:], in_=c[:], func=ACT.Square)
+            if USE_TACC:
+                mB = sum_over_experts(c2, "mB")
+                rT = spool.tile([P, OC], F32, name="rT")
+                nc.scalar.activation(out=rT[:], in_=mB[:, 0:256], func=ACT.Abs_reciprocal_sqrt, scale=0.25)
+                r = back(mB, rT)
+            else:
+                q2 = spool.tile([P, 2, OC], F32, name="q2")
+                nc.vector.tensor_tensor(out=q2[:], in0=c2[:, 0:2, :], in1=c2[:, 2:4, :], op=ALU.add)
+                q4 = spool.tile([P, OC], F32, name="q4")
+                nc.vector.tensor_tensor(out=q4[:], in0=q2[:, 0, :], in1=q2[:, 1, :], op=ALU.add)
+                rs = spool.tile([P, OC], F32, name="rs")
+                nc.scalar.activation(out=rs[:], in_=q4[:], func=ACT.Abs_reciprocal_sqrt, scale=0.25)
+                r = rs[:]
+            u = upool.tile([P, HN, OC], F32, name="u")
             for n in range(HN):
                 nc.vector.scalar_tensor_tensor(
                     out=u[:, n, :], in0=r, scalar=1.0e8, in1=c[:, n, :], op0=ALU.min, op1=ALU.mult,
                     accum_out=su[:, t, n : n + 1],
                 )
-            U[t] = u
+            junk = spool.tile([P, OC], F32, name="junk")
+            for n in range(HN):
+                nc.scalar.activation(out=junk[:], in_=u[:, n, :], func=ACT.Square, accum_out=sq[:, t, n : n + 1])
+            utiles[t] = u
 
-        def e_usq(t, n):
-            junk = work.tile([P, OC], F32, name="junk")
-            nc.scalar.activation(out=junk[:], in_=U[t][:, n, :], func=ACT.Square, accum_out=sq[:, t, n : n + 1])
-
-        def small(name):
-            return work.tile([P, GROUP, HN], F32, name=name)
-
-        def fin(gi, step):
+        def finish(gi):
             t0 = gi * GROUP
             ts = slice(t0, t0 + GROUP)
-            if step == 0:
-                mu = small("mu")
-                nc.vector.tensor_scalar_mul(out=mu[:], in0=su[:, ts, :], scalar1=1.0 / OC)
-                FIN[gi] = {"mu": mu}
-            f = FIN[gi]
-            if step == 1:
-                m2 = small("m2")
-                nc.vector.tensor_tensor(out=m2[:], in0=f["mu"][:], in1=f["mu"][:], op=ALU.mult)
-                f["m2"] = m2
-            if step == 2:
-                var = small("var")
-                nc.vector.scalar_tensor_tensor(
-                    out=var[:], in0=sq[:, ts, :], scalar=1.0 / OC, in1=f["m2"][:], op0=ALU.mult, op1=ALU.subtract
-                )
-                f["var"] = var
-            if step == 3:
-                a = small("a")
-                nc.scalar.activation(out=a[:], in_=f["var"][:], func=ACT.Abs_reciprocal_sqrt)
-                f["a"] = a
-            if step == 4:
-                a4 = small("a4")
-                nc.vector.tensor_scalar(out=a4[:], in0=f["a"][:], scalar1=1.0e8, scalar2=0.25, op0=ALU.min, op1=ALU.mult)
-                f["a4"] = a4
-            if step == 5:
-                am = small("am")
-                nc.vector.scalar_tensor_tensor(
-                    out=am[:], in0=f["mu"][:], scalar=-1.0, in1=f["a4"][:], op0=ALU.mult, op1=ALU.mult
-                )
-                f["am"] = am
-                dl = work.tile([P, GROUP, 3], F32, name="dl")
-                nc.vector.tensor_tensor(
-                    out=dl[:], in0=f["a4"][:, :, 0:3], in1=f["a4"][:, :, 3:4].to_broadcast([P, GROUP, 3]), op=ALU.subtract
-                )
-                f["dl"] = dl
-            if step == 6:
-                nk = work.tile([P, GROUP], F32, name="nk")
-                nc.vector.tensor_reduce(out=nk[:], in_=f["am"][:], axis=AX.X, op=ALU.add)
-                f["nk"] = nk
-                ob = work.tile([P, GROUP, OC], F32, name="ob")
-                f["ob"] = ob
-
-        def fin_first(gi, k):
-            f = FIN[gi]
-            f0 = work.tile([P, OC], F32, name="f0")
-            nc.scalar.activation(
-                out=f0[:], in_=U[gi * GROUP + k][:, 0, :], func=ACT.Identity,
-                scale=f["dl"][:, k, 0:1], bias=f["nk"][:, k : k + 1],
-            )
-            f[("f0", k)] = f0
-
-        def fin_rest(gi, k):
-            f = FIN[gi]
-            u = U.pop(gi * GROUP + k)
-            f1 = work.tile([P, OC], F32, name="f1")
+            mu = spool.tile([P, GROUP, HN], F32, name="mu")
+            nc.vector.tensor_scalar_mul(out=mu[:], in0=su[:, ts, :], scalar1=1.0 / OC)
+            m2 = spool.tile([P, GROUP, HN], F32, name="m2")
+            nc.vector.tensor_tensor(out=m2[:], in0=mu[:], in1=mu[:], op=ALU.mult)
+            var = spool.tile([P, GROUP, HN], F32, name="var")
             nc.vector.scalar_tensor_tensor(
-                out=f1[:], in0=u[:, 1, :], scalar=f["dl"][:, k, 1:2], in1=f[("f0", k)][:], op0=ALU.mult, op1=ALU.add
+                out=var[:], in0=sq[:, ts, :], scalar=1.0 / OC, in1=m2[:], op0=ALU.mult, op1=ALU.subtract
             )
-            nc.vector.scalar_tensor_tensor(
-                out=f["ob"][:, k, :], in0=u[:, 2, :], scalar=f["dl"][:, k, 2:3], in1=f1[:], op0=ALU.mult, op1=ALU.add
+            a = spool.tile([P, GROUP, HN], F32, name="a")
+            nc.scalar.activation(out=a[:], in_=var[:], func=ACT.Abs_reciprocal_sqrt)
+            a4 = spool.tile([P, GROUP, HN], F32, name="a4")
+            nc.vector.tensor_scalar(out=a4[:], in0=a[:], scalar1=1.0e8, scalar2=0.25, op0=ALU.min, op1=ALU.mult)
+            am = spool.tile([P, GROUP, HN], F32, name="am")
+            nc.vector.scalar_tensor_tensor(out=am[:], in0=mu[:], scalar=-1.0, in1=a4[:], op0=ALU.mult, op1=ALU.mult)
+            nk = spool.tile([P, GROUP], F32, name="nk")
+            nc.vector.tensor_reduce(out=nk[:], in_=am[:], axis=AX.X, op=ALU.add)
+            dl = spool.tile([P, GROUP, 3], F32, name="dl")
+            nc.vector.tensor_tensor(
+                out=dl[:], in0=a4[:, :, 0:3], in1=a4[:, :, 3:4].to_broadcast([P, GROUP, 3]), op=ALU.subtract
             )
+            ob = opool.tile([P, GROUP, OC], F32, name="ob")
+            for k in range(GROUP):
+                u = utiles.pop(t0 + k)
+                f0 = spool.tile([P, OC], F32, name="f0")
+                nc.scalar.activation(
+                    out=f0[:], in_=u[:, 0, :], func=ACT.Identity, scale=dl[:, k, 0:1], bias=nk[:, k : k + 1]
+                )
+                f1 = spool.tile([P, OC], F32, name="f1")
+                nc.vector.scalar_tensor_tensor(
+                    out=f1[:], in0=u[:, 1, :], scalar=dl[:, k, 1:2], in1=f0[:], op0=ALU.mult, op1=ALU.add
+                )
+                nc.vector.scalar_tensor_tensor(
+                    out=ob[:, k, :], in0=u[:, 2, :], scalar=dl[:, k, 2:3], in1=f1[:], op0=ALU.mult, op1=ALU.add
+                )
+            nc.sync.dma_start(out=out_view[:, ts, :], in_=ob[:])
 
-        def fin_store(gi):
-            f = FIN.pop(gi)
-            nc.sync.dma_start(out=out_view[:, gi * GROUP : (gi + 1) * GROUP, :], in_=f["ob"][:])
-
-        def bank(x):
-            return 0 <= x < NS
-
-        def tile_at(x):
-            return x % HN == 0 and 0 <= x // HN < NT
-
-        last = 16 * (NG - 1) + 35 + 13
-        for tau in range(last + 1):
-            if tau % HN == 0 and tau // HN + AHEAD < NT:
-                load(tau // HN + AHEAD)
-            if bank(tau - 5):
-                mx(tau - 5)
-            if tile_at(tau - 10):
-                e_sum((tau - 10) // HN)
-            if tile_at(tau - 12):
-                e_nmback((tau - 12) // HN)
-            if tile_at(tau - 15):
-                e_q((tau - 15) // HN)
-            if tile_at(tau - 17):
-                e_rback((tau - 17) // HN)
-            if bank(tau - 1):
-                transposes(tau - 1)
-            if tile_at(tau - 11):
-                e_nm((tau - 11) // HN)
-            if tile_at(tau - 16):
-                e_r((tau - 16) // HN)
-            if bank(tau - 6):
-                weigh(tau - 6)
-            if bank(tau - 2):
-                leak_times(tau - 2)
-            if tile_at(tau - 14):
-                e_square((tau - 14) // HN)
-            for n in range(HN):
-                if tile_at(tau - 19 - n):
-                    e_usq((tau - 19 - n) // HN, n)
-            if bank(tau - 4):
-                quantise(tau - 4)
-            if bank(tau):
-                flip(tau)
-            if tau == 0:
-                prep_w()
-            if bank(tau - 3):
-                take_max(tau - 3)
-            if tile_at(tau - 13):
-                e_centre((tau - 13) // HN)
-            if tile_at(tau - 18):
-                e_u((tau - 18) // HN)
-            x = tau - 35
-            if x >= 0:
-                gi, step = divmod(x, 16)
-                if gi < NG and step <= 6:
-                    fin(gi, step)
-                if gi < NG and 7 <= step <= 10:
-                    fin_first(gi, step - 7)
-                if gi < NG and 8 <= step <= 11:
-                    fin_rest(gi, step - 8)
-                if gi < NG and step == 13:
-                    fin_store(gi)
+        for i in range(NT + LAG):
+            if i + 3 < NT:
+                load(i + 3)
+            if i < NT:
+                main(i)
+            j = i - LAG
+            if j >= 0:
+                epi(j)
+                if j % GROUP == GROUP - 1:
+                    finish(j // GROUP)

@@ -15,31 +15,54 @@ AX = mybir.AxisListType
 P = 128
 B, HN, HM, OC = 4096, 4, 1024, 256
 NT = B // P
+NS = NT * HN
 GROUP = 4
+NG = NT // GROUP
 FLOPS = 2 * B * HN * HM * OC
 
-USE_TACC = True
-LAG = 1
+PIN = True
+AHEAD = 3
+ORDER = [
+    ("qs", 21),
+    ("usq1", 28),
+    ("usq0", 31),
+    ("nmb", 18),
+    ("T", (5, 5)),
+    ("quant", (9, 8)),
+    ("flip", (0, 1)),
+    ("ce0", 18),
+    ("u3", 23),
+    ("L", (7, 6)),
+    ("usq3", 25),
+    ("u2", 23),
+    ("mx", (10, 9)),
+    ("u0", 23),
+    ("usq2", 26),
+    ("weigh", (11, 11)),
+    ("sq0", 19),
+    ("r", 22),
+    ("max", (7, 7)),
+    ("rb", 22),
+    ("nm", 16),
+    ("sum", 15),
+    ("u1", 23),
+]
+FIN_BASE = 44
 
 
 def l_on_vector(t, n):
-    return n == 3 and t % 2 == 1
+    return n == 3 and t % 4 != 3
 
 
 def tile_tensormoe_pb_t_kernel(tc, h_pre, W_mo, weights_n, leak_n, out):
     nc = tc.nc
     with ExitStack() as ctx:
+        if PIN:
+            ctx.enter_context(tc.manual_schedule())
         const = ctx.enter_context(tc.tile_pool(name="const", bufs=1))
-        hpool = ctx.enter_context(tc.tile_pool(name="hpool", bufs=4))
-        lpool = ctx.enter_context(tc.tile_pool(name="lpool", bufs=4))
-        gpool = ctx.enter_context(tc.tile_pool(name="gpool", bufs=2))
-        qpool = ctx.enter_context(tc.tile_pool(name="qpool", bufs=2))
-        epool = ctx.enter_context(tc.tile_pool(name="epool", bufs=2))
-        upool = ctx.enter_context(tc.tile_pool(name="upool", bufs=2 * GROUP))
-        spool = ctx.enter_context(tc.tile_pool(name="spool", bufs=2))
-        opool = ctx.enter_context(tc.tile_pool(name="opool", bufs=2))
-        xpsum = ctx.enter_context(tc.psum_pool(name="xpsum", bufs=3))
-        ypsum = ctx.enter_context(tc.psum_pool(name="ypsum", bufs=3))
+        work = ctx.enter_context(tc.tile_pool(name="work", bufs=2))
+        xpsum = ctx.enter_context(tc.psum_pool(name="xpsum", bufs=4))
+        ypsum = ctx.enter_context(tc.psum_pool(name="ypsum", bufs=2))
         mpsum = ctx.enter_context(tc.psum_pool(name="mpsum", bufs=1))
 
         h_view = h_pre.rearrange("(p t) n m -> p t (n m)", t=NT)
@@ -50,12 +73,26 @@ def tile_tensormoe_pb_t_kernel(tc, h_pre, W_mo, weights_n, leak_n, out):
         wtb = const.tile([P, NT * HN], BF16)
         nc.sync.dma_start(out=wtb[:], in_=weights_n.rearrange("(p t) n -> p (t n)", t=NT))
 
-        htiles = {}
+        H = {}
+        X = {}
+        L = {}
+        G = {}
+        Q = {}
+        Y = {}
+        Z = {}
+        C = {}
+        C2 = {}
+        MA = {}
+        MB = {}
+        TT = {}
+        U = {}
+        FIN = {}
+        UC = {}
 
         def load(t):
-            hsb = hpool.tile([P, HN * HM], BF16, name="hsb")
+            hsb = work.tile([P, HN * HM], BF16, name="hsb", bufs=6)
             nc.sync.dma_start(out=hsb[:], in_=h_view[:, t, :])
-            htiles[t] = hsb
+            H[t] = hsb
 
         load(0)
         wraw = const.tile([P, 16 * 512], BF16)
@@ -63,8 +100,8 @@ def tile_tensormoe_pb_t_kernel(tc, h_pre, W_mo, weights_n, leak_n, out):
             out=wraw[:].rearrange("p (a r) -> p a r", a=16),
             in_=W_mo.rearrange("n (g u p e) o -> p (n g u) (e o)", g=2, u=2, p=P, e=2),
         )
-        load(1)
-        load(2)
+        for t in range(1, AHEAD):
+            load(t)
 
         ident = const.tile([P, P], F32)
         make_identity(nc, ident[:])
@@ -81,73 +118,99 @@ def tile_tensormoe_pb_t_kernel(tc, h_pre, W_mo, weights_n, leak_n, out):
             in1=sg[:].unsqueeze(1).to_broadcast([P, NT, HN]),
             op=ALU.mult,
         )
-
         wgrp = const.tile([P, 8192], BF16, align_bytes=64)
-        wsrc = wraw[:].rearrange("p (a t o) -> p a o t", a=8, t=4, o=OC)
-        wdst = wgrp[:].rearrange("p (a o t) -> p a o t", a=8, t=4, o=OC)
-        nc.vector.tensor_copy(out=wdst[:, 0:4], in_=wsrc[:, 0:4])
-        nc.scalar.copy(out=wdst[:, 4:8], in_=wsrc[:, 4:8])
-        wcodes = const.tile([P, 2304], U32, align_bytes=64)
-        wscales = const.tile([P, 2304], U8, align_bytes=64)
-        nc.vector.quantize_mx(out=wcodes[:, 2048:2304].bitcast(FP8X4), scales=wscales[:, 2048:2304], in_=wgrp[:, 0:1024])
-        for hf in range(2):
-            nc.vector.quantize_mx(
-                out=wcodes[:, hf * 1024 : (hf + 1) * 1024].bitcast(FP8X4),
-                scales=wscales[:, hf * 1024 : (hf + 1) * 1024],
-                in_=wgrp[:, hf * 4096 : (hf + 1) * 4096],
-            )
-
+        wcodes = const.tile([P, 2048], U32, align_bytes=64)
+        wscales = const.tile([P, 2048], U8, align_bytes=64)
         su = const.tile([P, NT, HN], F32)
         sq = const.tile([P, NT, HN], F32)
 
-        ytiles = {}
-        utiles = {}
-
-        def main(t):
-            hsb = htiles.pop(t)
-            for n in range(HN):
-                sl = hsb[:, n * HM : (n + 1) * HM]
-                nc.vector.tensor_scalar(out=sl, in0=sl, scalar1=sg[:, n : n + 1], scalar2=None, op0=ALU.mult)
-            hw = hsb[:].bitcast(F32)
-            grp = gpool.tile([P, HN * HM], BF16, name="grp", align_bytes=64)
-            for n in range(HN):
-                xt = xpsum.tile([P, 512], F32, name="xt")
-                for u in range(2):
-                    for g in range(2):
-                        j = u * 2 + g
-                        c0 = n * 512 + g * 256 + u * 128
-                        nc.tensor.transpose(xt[:, j * P : (j + 1) * P], hw[:, c0 : c0 + P], ident[:])
-                xb = xt[:].bitcast(BF16)
-                lt = lpool.tile([P, HM], BF16, name="lt")
-                if l_on_vector(t, n):
-                    nc.vector.tensor_scalar(out=lt[:], in0=xb, scalar1=lk[:, n : n + 1], scalar2=None, op0=ALU.mult)
-                else:
-                    nc.scalar.activation(out=lt[:], in_=xb, func=ACT.Copy, scale=lk[:, n : n + 1])
-                nc.vector.tensor_tensor(
-                    out=grp[:, n * HM : (n + 1) * HM].rearrange("p (w u e) -> p w u e", u=2, e=2),
-                    in0=lt[:].rearrange("p (u w e) -> p w u e", u=2, e=2),
-                    in1=xb.rearrange("p (u w e) -> p w u e", u=2, e=2),
-                    op=ALU.max,
+        def prep_w():
+            wsrc = wraw[:].rearrange("p (a t o) -> p a o t", a=8, t=4, o=OC)
+            wdst = wgrp[:].rearrange("p (a o t) -> p a o t", a=8, t=4, o=OC)
+            nc.scalar.copy(out=wdst[:, 5:8], in_=wsrc[:, 5:8])
+            nc.vector.tensor_copy(out=wdst[:, 0:5], in_=wsrc[:, 0:5])
+            for hf in range(2):
+                nc.vector.quantize_mx(
+                    out=wcodes[:, hf * 1024 : (hf + 1) * 1024].bitcast(FP8X4),
+                    scales=wscales[:, hf * 1024 : (hf + 1) * 1024],
+                    in_=wgrp[:, hf * 4096 : (hf + 1) * 4096],
                 )
-            codes = qpool.tile([P, HN * 256], U32, name="codes", align_bytes=64)
-            scales = qpool.tile([P, HN * 256], U8, name="scales", align_bytes=64)
-            nc.vector.quantize_mx(out=codes[:].bitcast(FP8X4), scales=scales[:], in_=grp[:])
-            ys = []
-            for n in range(HN):
-                y = ypsum.tile([P, 512], F32, name="y")
+
+        def flip(s):
+            t, n = divmod(s, HN)
+            sl = H[t][:, n * HM : (n + 1) * HM]
+            nc.vector.tensor_scalar(out=sl, in0=sl, scalar1=sg[:, n : n + 1], scalar2=None, op0=ALU.mult)
+
+        def transposes(s):
+            t, n = divmod(s, HN)
+            hw = H[t][:].bitcast(F32)
+            xt = xpsum.tile([P, 512], F32, name="xt")
+            for u in range(2):
                 for g in range(2):
-                    a = n * 2 + g
-                    nc.tensor.matmul_mx(
-                        out=y[:],
-                        lhsT=codes[:, a * P : (a + 1) * P].bitcast(FP8X4),
-                        lhsT_scale=scales[:, a * P : (a + 1) * P],
-                        rhs=wcodes[:, a * OC : a * OC + 512].bitcast(FP8X4),
-                        rhs_scale=wscales[:, a * OC : a * OC + 512],
-                        start=(g == 0),
-                        stop=(g == 1),
-                    )
-                ys.append(y)
-            ytiles[t] = ys
+                    j = u * 2 + g
+                    c0 = n * 512 + g * 256 + u * 128
+                    nc.tensor.transpose(xt[:, j * P : (j + 1) * P], hw[:, c0 : c0 + P], ident[:])
+            X[s] = xt
+            if n == HN - 1:
+                H.pop(t)
+
+        def leak_times(s):
+            t, n = divmod(s, HN)
+            xb = X[s][:].bitcast(BF16)
+            lt = work.tile([P, HM], BF16, name="lt", bufs=4)
+            if l_on_vector(t, n):
+                nc.vector.tensor_scalar(out=lt[:], in0=xb, scalar1=lk[:, n : n + 1], scalar2=None, op0=ALU.mult)
+            else:
+                nc.scalar.activation(out=lt[:], in_=xb, func=ACT.Copy, scale=lk[:, n : n + 1])
+            L[s] = lt
+
+        def take_max(s):
+            xb = X.pop(s)[:].bitcast(BF16)
+            lt = L.pop(s)
+            grp = work.tile([P, HM], BF16, name="grp", bufs=4, align_bytes=64)
+            nc.vector.tensor_tensor(
+                out=grp[:].rearrange("p (w u e) -> p w u e", u=2, e=2),
+                in0=lt[:].rearrange("p (u w e) -> p w u e", u=2, e=2),
+                in1=xb.rearrange("p (u w e) -> p w u e", u=2, e=2),
+                op=ALU.max,
+            )
+            G[s] = grp
+
+        def quantise(s):
+            grp = G.pop(s)
+            codes = work.tile([P, 256], U32, name="codes", bufs=4, align_bytes=64)
+            scales = work.tile([P, 256], U8, name="scales", bufs=4, align_bytes=64)
+            nc.vector.quantize_mx(out=codes[:].bitcast(FP8X4), scales=scales[:], in_=grp[:])
+            Q[s] = (codes, scales)
+
+        def mx(s):
+            t, n = divmod(s, HN)
+            codes, scales = Q.pop(s)
+            if n % 2 == 0:
+                y = ypsum.tile([P, 2, OC], F32, name="y")
+                Y[s // 2] = y
+            y = Y[s // 2]
+            for g in range(2):
+                a = n * 2 + g
+                nc.tensor.matmul_mx(
+                    out=y[:, n % 2, :],
+                    lhsT=codes[:, g * P : (g + 1) * P].bitcast(FP8X4),
+                    lhsT_scale=scales[:, g * P : (g + 1) * P],
+                    rhs=wcodes[:, a * OC : (a + 1) * OC].bitcast(FP8X4),
+                    rhs_scale=wscales[:, a * OC : (a + 1) * OC],
+                    start=(g == 0),
+                    stop=(g == 1),
+                )
+
+        def weigh(s):
+            t, n = divmod(s, HN)
+            if n == 0:
+                z = work.tile([P, HN, OC], F32, name="z", bufs=3)
+                Z[t] = z
+            y = Y[s // 2]
+            nc.scalar.activation(out=Z[t][:, n, :], in_=y[:, n % 2, :], func=ACT.Copy, scale=wp[:, t, n : n + 1])
+            if n % 2 == 1:
+                Y.pop(s // 2)
 
         def sum_over_experts(src, tagname):
             m = mpsum.tile([P, 512], F32, name=tagname)
@@ -163,104 +226,170 @@ def tile_tensormoe_pb_t_kernel(tc, h_pre, W_mo, weights_n, leak_n, out):
                     )
             return m
 
-        def back(m, srcT):
+        def back(m, src_t):
             for hf in range(2):
-                nc.tensor.transpose(m[:, 256 + hf * P : 256 + (hf + 1) * P], srcT[:, hf * P : (hf + 1) * P], ident[:])
-            return m[:, 256:512]
+                nc.tensor.transpose(m[:, 256 + hf * P : 256 + (hf + 1) * P], src_t[:, hf * P : (hf + 1) * P], ident[:])
 
-        def epi(t):
-            ys = ytiles.pop(t)
-            z = epool.tile([P, HN, OC], F32, name="z")
-            for n in range(HN):
-                nc.scalar.activation(out=z[:, n, :], in_=ys[n][:, 0:OC], func=ACT.Copy, scale=wp[:, t, n : n + 1])
-            c = epool.tile([P, HN, OC], F32, name="c")
-            if USE_TACC:
-                mA = sum_over_experts(z, "mA")
-                nmT = spool.tile([P, OC], F32, name="nmT")
-                nc.scalar.activation(out=nmT[:], in_=mA[:, 0:256], func=ACT.Copy, scale=-0.25)
-                nm = back(mA, nmT)
-                nc.vector.tensor_tensor(out=c[:], in0=z[:], in1=nm.unsqueeze(1).to_broadcast([P, HN, OC]), op=ALU.add)
-            else:
-                s2 = spool.tile([P, 2, OC], F32, name="s2")
-                nc.vector.tensor_tensor(out=s2[:], in0=z[:, 0:2, :], in1=z[:, 2:4, :], op=ALU.add)
-                s4 = spool.tile([P, OC], F32, name="s4")
-                nc.vector.tensor_tensor(out=s4[:], in0=s2[:, 0, :], in1=s2[:, 1, :], op=ALU.add)
-                nc.vector.scalar_tensor_tensor(
-                    out=c[:], in0=s4[:].unsqueeze(1).to_broadcast([P, HN, OC]), scalar=-0.25, in1=z[:],
-                    op0=ALU.mult, op1=ALU.add,
-                )
-            c2 = epool.tile([P, HN, OC], F32, name="c2")
-            nc.scalar.activation(out=c2[:], in_=c[:], func=ACT.Square)
-            if USE_TACC:
-                mB = sum_over_experts(c2, "mB")
-                rT = spool.tile([P, OC], F32, name="rT")
-                nc.scalar.activation(out=rT[:], in_=mB[:, 0:256], func=ACT.Abs_reciprocal_sqrt, scale=0.25)
-                r = back(mB, rT)
-            else:
-                q2 = spool.tile([P, 2, OC], F32, name="q2")
-                nc.vector.tensor_tensor(out=q2[:], in0=c2[:, 0:2, :], in1=c2[:, 2:4, :], op=ALU.add)
-                q4 = spool.tile([P, OC], F32, name="q4")
-                nc.vector.tensor_tensor(out=q4[:], in0=q2[:, 0, :], in1=q2[:, 1, :], op=ALU.add)
-                rs = spool.tile([P, OC], F32, name="rs")
-                nc.scalar.activation(out=rs[:], in_=q4[:], func=ACT.Abs_reciprocal_sqrt, scale=0.25)
-                r = rs[:]
-            u = upool.tile([P, HN, OC], F32, name="u")
-            for n in range(HN):
-                nc.vector.scalar_tensor_tensor(
-                    out=u[:, n, :], in0=r, scalar=1.0e8, in1=c[:, n, :], op0=ALU.min, op1=ALU.mult,
-                    accum_out=su[:, t, n : n + 1],
-                )
-            junk = spool.tile([P, OC], F32, name="junk")
-            for n in range(HN):
-                nc.scalar.activation(out=junk[:], in_=u[:, n, :], func=ACT.Square, accum_out=sq[:, t, n : n + 1])
-            utiles[t] = u
+        def e_sum(t):
+            MA[t] = sum_over_experts(Z[t], "mA")
 
-        def finish(gi):
+        def e_nm(t):
+            nmt = work.tile([P, OC], F32, name="nmt")
+            nc.scalar.activation(out=nmt[:], in_=MA[t][:, 0:256], func=ACT.Copy, scale=-0.25)
+            TT[t] = nmt
+
+        def e_nmback(t):
+            back(MA[t], TT.pop(t))
+
+        def e_centre(t):
+            c = work.tile([P, HN, OC], F32, name="c", bufs=3)
+            nm = MA.pop(t)[:, 256:512]
+            nc.vector.tensor_tensor(
+                out=c[:], in0=Z.pop(t)[:], in1=nm.unsqueeze(1).to_broadcast([P, HN, OC]), op=ALU.add
+            )
+            C[t] = c
+
+        def e_square(t):
+            c2 = work.tile([P, HN, OC], F32, name="c2")
+            nc.scalar.activation(out=c2[:], in_=C[t][:], func=ACT.Square)
+            C2[t] = c2
+
+        def e_q(t):
+            MB[t] = sum_over_experts(C2.pop(t), "mB")
+
+        def e_r(t):
+            rt = work.tile([P, OC], F32, name="rt")
+            nc.scalar.activation(out=rt[:], in_=MB[t][:, 0:256], func=ACT.Abs_reciprocal_sqrt, scale=0.25)
+            TT[t] = rt
+
+        def e_rback(t):
+            back(MB[t], TT.pop(t))
+
+        def e_u(t, n):
+            if t not in U:
+                u = work.tile([P, HN, OC], F32, name="u", bufs=10)
+                U[t] = u
+                UC[t] = 0
+            nc.vector.scalar_tensor_tensor(
+                out=U[t][:, n, :], in0=MB[t][:, 256:512], scalar=1.0e8, in1=C[t][:, n, :], op0=ALU.min, op1=ALU.mult,
+                accum_out=su[:, t, n : n + 1],
+            )
+            UC[t] += 1
+            if UC[t] == HN:
+                MB.pop(t)
+                C.pop(t)
+
+        def e_usq(t, n):
+            junk = work.tile([P, OC], F32, name="junk")
+            nc.scalar.activation(out=junk[:], in_=U[t][:, n, :], func=ACT.Square, accum_out=sq[:, t, n : n + 1])
+
+        def small(name):
+            return work.tile([P, GROUP, HN], F32, name=name)
+
+        def fin(gi, step):
             t0 = gi * GROUP
             ts = slice(t0, t0 + GROUP)
-            mu = spool.tile([P, GROUP, HN], F32, name="mu")
-            nc.vector.tensor_scalar_mul(out=mu[:], in0=su[:, ts, :], scalar1=1.0 / OC)
-            m2 = spool.tile([P, GROUP, HN], F32, name="m2")
-            nc.vector.tensor_tensor(out=m2[:], in0=mu[:], in1=mu[:], op=ALU.mult)
-            var = spool.tile([P, GROUP, HN], F32, name="var")
-            nc.vector.scalar_tensor_tensor(
-                out=var[:], in0=sq[:, ts, :], scalar=1.0 / OC, in1=m2[:], op0=ALU.mult, op1=ALU.subtract
-            )
-            a = spool.tile([P, GROUP, HN], F32, name="a")
-            nc.scalar.activation(out=a[:], in_=var[:], func=ACT.Abs_reciprocal_sqrt)
-            a4 = spool.tile([P, GROUP, HN], F32, name="a4")
-            nc.vector.tensor_scalar(out=a4[:], in0=a[:], scalar1=1.0e8, scalar2=0.25, op0=ALU.min, op1=ALU.mult)
-            am = spool.tile([P, GROUP, HN], F32, name="am")
-            nc.vector.scalar_tensor_tensor(out=am[:], in0=mu[:], scalar=-1.0, in1=a4[:], op0=ALU.mult, op1=ALU.mult)
-            nk = spool.tile([P, GROUP], F32, name="nk")
-            nc.vector.tensor_reduce(out=nk[:], in_=am[:], axis=AX.X, op=ALU.add)
-            dl = spool.tile([P, GROUP, 3], F32, name="dl")
-            nc.vector.tensor_tensor(
-                out=dl[:], in0=a4[:, :, 0:3], in1=a4[:, :, 3:4].to_broadcast([P, GROUP, 3]), op=ALU.subtract
-            )
-            ob = opool.tile([P, GROUP, OC], F32, name="ob")
-            for k in range(GROUP):
-                u = utiles.pop(t0 + k)
-                f0 = spool.tile([P, OC], F32, name="f0")
-                nc.scalar.activation(
-                    out=f0[:], in_=u[:, 0, :], func=ACT.Identity, scale=dl[:, k, 0:1], bias=nk[:, k : k + 1]
-                )
-                f1 = spool.tile([P, OC], F32, name="f1")
+            if step == 0:
+                mu = small("mu")
+                nc.vector.tensor_scalar_mul(out=mu[:], in0=su[:, ts, :], scalar1=1.0 / OC)
+                FIN[gi] = {"mu": mu}
+            f = FIN[gi]
+            if step == 1:
+                m2 = small("m2")
+                nc.vector.tensor_tensor(out=m2[:], in0=f["mu"][:], in1=f["mu"][:], op=ALU.mult)
+                f["m2"] = m2
+            if step == 2:
+                var = small("var")
                 nc.vector.scalar_tensor_tensor(
-                    out=f1[:], in0=u[:, 1, :], scalar=dl[:, k, 1:2], in1=f0[:], op0=ALU.mult, op1=ALU.add
+                    out=var[:], in0=sq[:, ts, :], scalar=1.0 / OC, in1=f["m2"][:], op0=ALU.mult, op1=ALU.subtract
                 )
+                f["var"] = var
+            if step == 3:
+                a = small("a")
+                nc.scalar.activation(out=a[:], in_=f["var"][:], func=ACT.Abs_reciprocal_sqrt)
+                f["a"] = a
+            if step == 4:
+                a4 = small("a4")
+                nc.vector.tensor_scalar(out=a4[:], in0=f["a"][:], scalar1=1.0e8, scalar2=0.25, op0=ALU.min, op1=ALU.mult)
+                f["a4"] = a4
+            if step == 5:
+                am = small("am")
                 nc.vector.scalar_tensor_tensor(
-                    out=ob[:, k, :], in0=u[:, 2, :], scalar=dl[:, k, 2:3], in1=f1[:], op0=ALU.mult, op1=ALU.add
+                    out=am[:], in0=f["mu"][:], scalar=-1.0, in1=f["a4"][:], op0=ALU.mult, op1=ALU.mult
                 )
-            nc.sync.dma_start(out=out_view[:, ts, :], in_=ob[:])
+                f["am"] = am
+                dl = work.tile([P, GROUP, 3], F32, name="dl")
+                nc.vector.tensor_tensor(
+                    out=dl[:], in0=f["a4"][:, :, 0:3], in1=f["a4"][:, :, 3:4].to_broadcast([P, GROUP, 3]), op=ALU.subtract
+                )
+                f["dl"] = dl
+            if step == 6:
+                nk = work.tile([P, GROUP], F32, name="nk")
+                nc.vector.tensor_reduce(out=nk[:], in_=f["am"][:], axis=AX.X, op=ALU.add)
+                f["nk"] = nk
+                ob = work.tile([P, GROUP, OC], F32, name="ob")
+                f["ob"] = ob
 
-        for i in range(NT + LAG):
-            if i + 3 < NT:
-                load(i + 3)
-            if i < NT:
-                main(i)
-            j = i - LAG
-            if j >= 0:
-                epi(j)
-                if j % GROUP == GROUP - 1:
-                    finish(j // GROUP)
+        def fin_first(gi, k):
+            f = FIN[gi]
+            f0 = work.tile([P, OC], F32, name="f0")
+            nc.scalar.activation(
+                out=f0[:], in_=U[gi * GROUP + k][:, 0, :], func=ACT.Identity,
+                scale=f["dl"][:, k, 0:1], bias=f["nk"][:, k : k + 1],
+            )
+            f[("f0", k)] = f0
+
+        def fin_rest(gi, k):
+            f = FIN[gi]
+            u = U.pop(gi * GROUP + k)
+            f1 = work.tile([P, OC], F32, name="f1")
+            nc.vector.scalar_tensor_tensor(
+                out=f1[:], in0=u[:, 1, :], scalar=f["dl"][:, k, 1:2], in1=f[("f0", k)][:], op0=ALU.mult, op1=ALU.add
+            )
+            nc.vector.scalar_tensor_tensor(
+                out=f["ob"][:, k, :], in0=u[:, 2, :], scalar=f["dl"][:, k, 2:3], in1=f1[:], op0=ALU.mult, op1=ALU.add
+            )
+
+        def fin_store(gi):
+            f = FIN.pop(gi)
+            nc.sync.dma_start(out=out_view[:, gi * GROUP : (gi + 1) * GROUP, :], in_=f["ob"][:])
+
+        bank_stage = {
+            "flip": flip, "T": transposes, "L": leak_times, "max": take_max, "quant": quantise, "mx": mx, "weigh": weigh,
+        }
+        tile_stage = {
+            "sum": e_sum, "nm": e_nm, "nmb": e_nmback, "ce0": e_centre, "sq0": e_square, "qs": e_q, "r": e_r, "rb": e_rback,
+        }
+
+        last = 16 * (NG - 1) + FIN_BASE + 13
+        for tau in range(last + 1):
+            if tau % HN == 0 and tau // HN + AHEAD < NT:
+                load(tau // HN + AHEAD)
+            for name, lag in ORDER:
+                if name in bank_stage:
+                    for par in range(2):
+                        s = tau - lag[par]
+                        if 0 <= s < NS and s % 2 == par:
+                            bank_stage[name](s)
+                            if name == "flip" and s == 0:
+                                prep_w()
+                else:
+                    x = tau - lag
+                    if x >= 0 and x % HN == 0 and x // HN < NT:
+                        if name in tile_stage:
+                            tile_stage[name](x // HN)
+                        elif name[0:3] == "usq":
+                            e_usq(x // HN, int(name[3]))
+                        else:
+                            e_u(x // HN, int(name[1]))
+            x = tau - FIN_BASE
+            if x >= 0:
+                gi, step = divmod(x, 16)
+                if gi < NG and step <= 6:
+                    fin(gi, step)
+                if gi < NG and 7 <= step <= 10:
+                    fin_first(gi, step - 7)
+                if gi < NG and 8 <= step <= 11:
+                    fin_rest(gi, step - 8)
+                if gi < NG and step == 13:
+                    fin_store(gi)

@@ -27,21 +27,21 @@ ORDER = [
     ("usq1", 28),
     ("usq0", 31),
     ("nmb", 18),
-    ("T", (5, 5)),
-    ("quant", (9, 8)),
-    ("flip", (0, 1)),
+    ("T", (5, 5, 5, 5)),
+    ("quant", (9, 8, 9, 8)),
+    ("flip", (0, 1, 0, 1)),
     ("ce0", 18),
     ("u3", 23),
-    ("L", (7, 6)),
+    ("L", (7, 6, 7, 6)),
     ("usq3", 25),
     ("u2", 23),
-    ("mx", (10, 9)),
+    ("mx", (12, 11, 10, 9)),
     ("u0", 23),
     ("usq2", 26),
-    ("weigh", (11, 11)),
+    ("weigh", (13, 12, 12, 11)),
     ("sq0", 19),
     ("r", 22),
-    ("max", (7, 7)),
+    ("max", (7, 7, 7, 7)),
     ("rb", 22),
     ("nm", 16),
     ("sum", 15),
@@ -178,8 +178,8 @@ def tile_tensormoe_pb_t_kernel(tc, h_pre, W_mo, weights_n, leak_n, out):
 
         def quantise(s):
             grp = G.pop(s)
-            codes = work.tile([P, 256], U32, name="codes", bufs=4, align_bytes=64)
-            scales = work.tile([P, 256], U8, name="scales", bufs=4, align_bytes=64)
+            codes = work.tile([P, 256], U32, name="codes", bufs=8, align_bytes=64)
+            scales = work.tile([P, 256], U8, name="scales", bufs=8, align_bytes=64)
             nc.vector.quantize_mx(out=codes[:].bitcast(FP8X4), scales=scales[:], in_=grp[:])
             Q[s] = (codes, scales)
 
@@ -367,9 +367,9 @@ def tile_tensormoe_pb_t_kernel(tc, h_pre, W_mo, weights_n, leak_n, out):
                 load(tau // HN + AHEAD)
             for name, lag in ORDER:
                 if name in bank_stage:
-                    for par in range(2):
-                        s = tau - lag[par]
-                        if 0 <= s < NS and s % 2 == par:
+                    for n in range(HN):
+                        s = tau - lag[n]
+                        if 0 <= s < NS and s % HN == n:
                             bank_stage[name](s)
                             if name == "flip" and s == 0:
                                 prep_w()

@@ -21,33 +21,60 @@ NG = NT // GROUP
 FLOPS = 2 * B * HN * HM * OC
 
 PIN = True
+XY_BUFS = 8
 AHEAD = 3
 ORDER = [
+    ("wr0", 3),
     ("qs", 21),
     ("usq1", 28),
+    ("wr2", 4),
+    ("wr3", 4),
     ("usq0", 31),
     ("nmb", 18),
     ("T", (5, 5, 5, 5)),
+    ("wr5", 4),
     ("quant", (9, 8, 9, 8)),
+    ("wr4", 6),
+    ("wq3", 8),
     ("flip", (0, 1, 0, 1)),
+    ("wr6", 5),
     ("ce0", 18),
     ("u3", 23),
+    ("wq2", 7),
+    ("wr1", 3),
+    ("wq1", 6),
     ("L", (7, 6, 7, 6)),
     ("usq3", 25),
+    ("wq0", 5),
     ("u2", 23),
-    ("mx", (12, 11, 10, 9)),
+    ("mx", (10, 9, 10, 9)),
     ("u0", 23),
     ("usq2", 26),
-    ("weigh", (13, 12, 12, 11)),
+    ("weigh", (11, 11, 11, 11)),
     ("sq0", 19),
     ("r", 22),
+    ("wr7", 6),
     ("max", (7, 7, 7, 7)),
     ("rb", 22),
     ("nm", 16),
     ("sum", 15),
     ("u1", 23),
 ]
+W_ON_SCALAR = (1, 3, 5, 7)
 FIN_BASE = 44
+ADVANCED = ("flip", "T", "L", "max", "quant")
+ADV_FROM = 96
+ADV_EVERY = 4
+ADV_MAX = 0
+GROUPS = [(4 * i, 4) for i in range(7)] + [(28, 3), (31, 1)]
+TAIL_FROM = 24
+USQ_T0 = 27
+USQ_T1 = 29
+USQ_T2 = 25
+USQ_T3 = 25
+FIN_T0 = 27
+FIN_T1 = 27
+FIN_T2 = 30
 
 
 def l_on_vector(t, n):
@@ -61,9 +88,8 @@ def tile_tensormoe_pb_t_kernel(tc, h_pre, W_mo, weights_n, leak_n, out):
             ctx.enter_context(tc.manual_schedule())
         const = ctx.enter_context(tc.tile_pool(name="const", bufs=1))
         work = ctx.enter_context(tc.tile_pool(name="work", bufs=2))
-        xpsum = ctx.enter_context(tc.psum_pool(name="xpsum", bufs=4))
-        ypsum = ctx.enter_context(tc.psum_pool(name="ypsum", bufs=2))
-        mpsum = ctx.enter_context(tc.psum_pool(name="mpsum", bufs=1))
+        xpsum = ctx.enter_context(tc.psum_pool(name="xpsum", bufs=XY_BUFS))
+        mpsum = xpsum
 
         h_view = h_pre.rearrange("(p t) n m -> p t (n m)", t=NT)
         out_view = out.rearrange("(p t) o -> p t o", t=NT)
@@ -89,22 +115,29 @@ def tile_tensormoe_pb_t_kernel(tc, h_pre, W_mo, weights_n, leak_n, out):
         FIN = {}
         UC = {}
 
-        def load(t):
+        def load(t, pieces):
             hsb = work.tile([P, HN * HM], BF16, name="hsb", bufs=6)
-            nc.sync.dma_start(out=hsb[:], in_=h_view[:, t, :])
+            w = HN * HM // pieces
+            for i in range(pieces):
+                nc.sync.dma_start(out=hsb[:, i * w : (i + 1) * w], in_=h_view[:, t, i * w : (i + 1) * w])
             H[t] = hsb
 
-        load(0)
+        load(0, HN)
         wraw = const.tile([P, 16 * 512], BF16)
         nc.sync.dma_start(
             out=wraw[:].rearrange("p (a r) -> p a r", a=16),
             in_=W_mo.rearrange("n (g u p e) o -> p (n g u) (e o)", g=2, u=2, p=P, e=2),
         )
         for t in range(1, AHEAD):
-            load(t)
+            load(t, 1)
 
         ident = const.tile([P, P], F32)
         make_identity(nc, ident[:])
+
+        one = const.tile([P, 1], F32)
+        nc.vector.memset(one[:], 1.0)
+        warm = const.tile([P, 1], F32)
+        nc.scalar.activation(out=warm[:], in_=one[:], func=ACT.Abs_reciprocal_sqrt)
 
         lk = const.tile([P, HN], F32)
         nc.vector.tensor_copy(out=lk[:], in_=lkb[:])
@@ -124,17 +157,21 @@ def tile_tensormoe_pb_t_kernel(tc, h_pre, W_mo, weights_n, leak_n, out):
         su = const.tile([P, NT, HN], F32)
         sq = const.tile([P, NT, HN], F32)
 
-        def prep_w():
-            wsrc = wraw[:].rearrange("p (a t o) -> p a o t", a=8, t=4, o=OC)
-            wdst = wgrp[:].rearrange("p (a o t) -> p a o t", a=8, t=4, o=OC)
-            nc.scalar.copy(out=wdst[:, 5:8], in_=wsrc[:, 5:8])
-            nc.vector.tensor_copy(out=wdst[:, 0:5], in_=wsrc[:, 0:5])
-            for hf in range(2):
-                nc.vector.quantize_mx(
-                    out=wcodes[:, hf * 1024 : (hf + 1) * 1024].bitcast(FP8X4),
-                    scales=wscales[:, hf * 1024 : (hf + 1) * 1024],
-                    in_=wgrp[:, hf * 4096 : (hf + 1) * 4096],
-                )
+        wsrc = wraw[:].rearrange("p (a t o) -> p a o t", a=8, t=4, o=OC)
+        wdst = wgrp[:].rearrange("p (a o t) -> p a o t", a=8, t=4, o=OC)
+
+        def w_regroup(a):
+            if a in W_ON_SCALAR:
+                nc.scalar.copy(out=wdst[:, a], in_=wsrc[:, a])
+            else:
+                nc.vector.tensor_copy(out=wdst[:, a], in_=wsrc[:, a])
+
+        def w_quantise(n):
+            nc.vector.quantize_mx(
+                out=wcodes[:, n * 512 : (n + 1) * 512].bitcast(FP8X4),
+                scales=wscales[:, n * 512 : (n + 1) * 512],
+                in_=wgrp[:, n * 2048 : (n + 1) * 2048],
+            )
 
         def flip(s):
             t, n = divmod(s, HN)
@@ -144,7 +181,7 @@ def tile_tensormoe_pb_t_kernel(tc, h_pre, W_mo, weights_n, leak_n, out):
         def transposes(s):
             t, n = divmod(s, HN)
             hw = H[t][:].bitcast(F32)
-            xt = xpsum.tile([P, 512], F32, name="xt")
+            xt = xpsum.tile([P, 512], F32, name="xt", tag="xy")
             for u in range(2):
                 for g in range(2):
                     j = u * 2 + g
@@ -187,7 +224,7 @@ def tile_tensormoe_pb_t_kernel(tc, h_pre, W_mo, weights_n, leak_n, out):
             t, n = divmod(s, HN)
             codes, scales = Q.pop(s)
             if n % 2 == 0:
-                y = ypsum.tile([P, 2, OC], F32, name="y")
+                y = xpsum.tile([P, 2, OC], F32, name="y", tag="xy")
                 Y[s // 2] = y
             y = Y[s // 2]
             for g in range(2):
@@ -213,7 +250,7 @@ def tile_tensormoe_pb_t_kernel(tc, h_pre, W_mo, weights_n, leak_n, out):
                 Y.pop(s // 2)
 
         def sum_over_experts(src, tagname):
-            m = mpsum.tile([P, 512], F32, name=tagname)
+            m = mpsum.tile([P, 512], F32, name=tagname, tag="xy")
             for hf in range(2):
                 for n in range(HN):
                     nc.tensor.matmul(
@@ -283,12 +320,13 @@ def tile_tensormoe_pb_t_kernel(tc, h_pre, W_mo, weights_n, leak_n, out):
             junk = work.tile([P, OC], F32, name="junk")
             nc.scalar.activation(out=junk[:], in_=U[t][:, n, :], func=ACT.Square, accum_out=sq[:, t, n : n + 1])
 
-        def small(name):
-            return work.tile([P, GROUP, HN], F32, name=name)
-
         def fin(gi, step):
-            t0 = gi * GROUP
-            ts = slice(t0, t0 + GROUP)
+            t0, size = GROUPS[gi]
+            ts = slice(t0, t0 + size)
+
+            def small(name):
+                return work.tile([P, size, HN], F32, name=name)
+
             if step == 0:
                 mu = small("mu")
                 nc.vector.tensor_scalar_mul(out=mu[:], in0=su[:, ts, :], scalar1=1.0 / OC)
@@ -318,30 +356,36 @@ def tile_tensormoe_pb_t_kernel(tc, h_pre, W_mo, weights_n, leak_n, out):
                     out=am[:], in0=f["mu"][:], scalar=-1.0, in1=f["a4"][:], op0=ALU.mult, op1=ALU.mult
                 )
                 f["am"] = am
-                dl = work.tile([P, GROUP, 3], F32, name="dl")
+                dl = work.tile([P, size, 3], F32, name="dl")
                 nc.vector.tensor_tensor(
-                    out=dl[:], in0=f["a4"][:, :, 0:3], in1=f["a4"][:, :, 3:4].to_broadcast([P, GROUP, 3]), op=ALU.subtract
+                    out=dl[:], in0=f["a4"][:, :, 0:3], in1=f["a4"][:, :, 3:4].to_broadcast([P, size, 3]), op=ALU.subtract
                 )
                 f["dl"] = dl
             if step == 6:
-                nk = work.tile([P, GROUP], F32, name="nk")
+                nk = work.tile([P, size], F32, name="nk")
                 nc.vector.tensor_reduce(out=nk[:], in_=f["am"][:], axis=AX.X, op=ALU.add)
                 f["nk"] = nk
-                ob = work.tile([P, GROUP, OC], F32, name="ob")
+                ob = work.tile([P, size, OC], F32, name="ob")
                 f["ob"] = ob
 
         def fin_first(gi, k):
             f = FIN[gi]
             f0 = work.tile([P, OC], F32, name="f0")
-            nc.scalar.activation(
-                out=f0[:], in_=U[gi * GROUP + k][:, 0, :], func=ACT.Identity,
-                scale=f["dl"][:, k, 0:1], bias=f["nk"][:, k : k + 1],
-            )
+            if GROUPS[gi][1] < GROUP:
+                nc.vector.tensor_scalar(
+                    out=f0[:], in0=U[GROUPS[gi][0] + k][:, 0, :], scalar1=f["dl"][:, k, 0:1], scalar2=f["nk"][:, k : k + 1],
+                    op0=ALU.mult, op1=ALU.add,
+                )
+            else:
+                nc.scalar.activation(
+                    out=f0[:], in_=U[GROUPS[gi][0] + k][:, 0, :], func=ACT.Identity,
+                    scale=f["dl"][:, k, 0:1], bias=f["nk"][:, k : k + 1],
+                )
             f[("f0", k)] = f0
 
         def fin_rest(gi, k):
             f = FIN[gi]
-            u = U.pop(gi * GROUP + k)
+            u = U.pop(GROUPS[gi][0] + k)
             f1 = work.tile([P, OC], F32, name="f1")
             nc.vector.scalar_tensor_tensor(
                 out=f1[:], in0=u[:, 1, :], scalar=f["dl"][:, k, 1:2], in1=f[("f0", k)][:], op0=ALU.mult, op1=ALU.add
@@ -352,7 +396,8 @@ def tile_tensormoe_pb_t_kernel(tc, h_pre, W_mo, weights_n, leak_n, out):
 
         def fin_store(gi):
             f = FIN.pop(gi)
-            nc.sync.dma_start(out=out_view[:, gi * GROUP : (gi + 1) * GROUP, :], in_=f["ob"][:])
+            t0, size = GROUPS[gi]
+            nc.sync.dma_start(out=out_view[:, t0 : t0 + size, :], in_=f["ob"][:])
 
         bank_stage = {
             "flip": flip, "T": transposes, "L": leak_times, "max": take_max, "quant": quantise, "mx": mx, "weigh": weigh,
@@ -361,35 +406,50 @@ def tile_tensormoe_pb_t_kernel(tc, h_pre, W_mo, weights_n, leak_n, out):
             "sum": e_sum, "nm": e_nm, "nmb": e_nmback, "ce0": e_centre, "sq0": e_square, "qs": e_q, "r": e_r, "rb": e_rback,
         }
 
-        last = 16 * (NG - 1) + FIN_BASE + 13
-        for tau in range(last + 1):
-            if tau % HN == 0 and tau // HN + AHEAD < NT:
-                load(tau // HN + AHEAD)
-            for name, lag in ORDER:
-                if name in bank_stage:
-                    for n in range(HN):
-                        s = tau - lag[n]
-                        if 0 <= s < NS and s % HN == n:
-                            bank_stage[name](s)
-                            if name == "flip" and s == 0:
-                                prep_w()
-                else:
-                    x = tau - lag
-                    if x >= 0 and x % HN == 0 and x // HN < NT:
-                        if name in tile_stage:
-                            tile_stage[name](x // HN)
-                        elif name[0:3] == "usq":
-                            e_usq(x // HN, int(name[3]))
-                        else:
-                            e_u(x // HN, int(name[1]))
-            x = tau - FIN_BASE
-            if x >= 0:
-                gi, step = divmod(x, 16)
-                if gi < NG and step <= 6:
-                    fin(gi, step)
-                if gi < NG and 7 <= step <= 10:
-                    fin_first(gi, step - 7)
-                if gi < NG and 8 <= step <= 11:
-                    fin_rest(gi, step - 8)
-                if gi < NG and step == 13:
-                    fin_store(gi)
+        events = {}
+
+        def at(step, rank, sub, fn, args):
+            if step not in events:
+                events[step] = []
+            events[step].append((rank, sub, len(events[step]), fn, args))
+
+        def advance(s):
+            return min(ADV_MAX, max(0, (s - ADV_FROM) // ADV_EVERY))
+
+        for rank, (name, lag) in enumerate(ORDER):
+            if name in bank_stage:
+                for s in range(NS):
+                    adv = advance(s) if name in ADVANCED else 0
+                    at(s + lag[s % HN] - adv, rank, s, bank_stage[name], (s,))
+            elif name[0:2] == "wr":
+                at(lag, rank, 0, w_regroup, (int(name[2]),))
+            elif name[0:2] == "wq":
+                at(lag, rank, 0, w_quantise, (int(name[2]),))
+            elif name in tile_stage:
+                for t in range(NT):
+                    at(HN * t + lag, rank, t, tile_stage[name], (t,))
+            elif name[0:3] == "usq":
+                n = int(name[3])
+                for t in range(NT):
+                    at(HN * t + (lag if t < TAIL_FROM else (USQ_T0, USQ_T1, USQ_T2, USQ_T3)[n]), rank, t, e_usq, (t, n))
+            else:
+                for t in range(NT):
+                    at(HN * t + lag, rank, t, e_u, (t, int(name[1])))
+        flip_lag = [lag for name, lag in ORDER if name == "flip"][0]
+        for t in range(AHEAD, NT):
+            at(HN * t + flip_lag[0] - advance(HN * t) - HN * AHEAD, -1, t, load, (t, 1))
+        after = len(ORDER)
+        for gi in range(len(GROUPS)):
+            t0, size = GROUPS[gi]
+            base = HN * (t0 + size - GROUP) + FIN_BASE
+            if t0 >= TAIL_FROM:
+                base = HN * (t0 + size - 1) + (FIN_T0, FIN_T1, FIN_T2)[gi - len(GROUPS) + 3]
+            for step in range(7):
+                at(base + step, after, gi, fin, (gi, step))
+            for k in range(size):
+                at(base + 7 + k, after + 1, gi, fin_first, (gi, k))
+                at(base + 8 + k, after + 2, gi, fin_rest, (gi, k))
+            at(base + 9 + size, after + 3, gi, fin_store, (gi,))
+        for step in sorted(events):
+            for rank, sub, k, fn, args in sorted(events[step], key=lambda ev: ev[0:3]):
+                fn(*args)

@@ -13,443 +13,349 @@ ACT = mybir.ActivationFunctionType
 AX = mybir.AxisListType
 
 P = 128
-B, HN, HM, OC = 4096, 4, 1024, 256
-NT = B // P
-NS = NT * HN
-GROUP = 4
-NG = NT // GROUP
-FLOPS = 2 * B * HN * HM * OC
-
-PIN = True
-XY_BUFS = 8
+ROWS, EXPERTS, HIDDEN, OUT_C = 4096, 4, 1024, 256
+TILES = ROWS // P
+BANKS = TILES * EXPERTS
+PASSES = HIDDEN // 512
 AHEAD = 3
-ORDER = [
-    ("wr0", 3),
-    ("qs", 21),
-    ("usq1", 28),
-    ("wr2", 4),
-    ("wr3", 4),
-    ("usq0", 31),
-    ("nmb", 18),
-    ("T", (5, 5, 5, 5)),
-    ("wr5", 4),
-    ("quant", (9, 8, 9, 8)),
-    ("wr4", 6),
-    ("wq3", 8),
-    ("flip", (0, 1, 0, 1)),
-    ("wr6", 5),
-    ("ce0", 18),
-    ("u3", 23),
-    ("wq2", 7),
-    ("wr1", 3),
-    ("wq1", 6),
-    ("L", (7, 6, 7, 6)),
-    ("usq3", 25),
-    ("wq0", 5),
-    ("u2", 23),
-    ("mx", (10, 9, 10, 9)),
-    ("u0", 23),
-    ("usq2", 26),
-    ("weigh", (11, 11, 11, 11)),
-    ("sq0", 19),
-    ("r", 22),
-    ("wr7", 6),
-    ("max", (7, 7, 7, 7)),
-    ("rb", 22),
-    ("nm", 16),
-    ("sum", 15),
-    ("u1", 23),
-]
-W_ON_SCALAR = (1, 3, 5, 7)
-FIN_BASE = 44
-ADVANCED = ("flip", "T", "L", "max", "quant")
-ADV_FROM = 96
-ADV_EVERY = 4
-ADV_MAX = 0
-GROUPS = [(4 * i, 4) for i in range(7)] + [(28, 3), (31, 1)]
-TAIL_FROM = 24
-USQ_T0 = 27
-USQ_T1 = 29
-USQ_T2 = 25
-USQ_T3 = 25
-FIN_T0 = 27
-FIN_T1 = 27
-FIN_T2 = 30
-
-
-def l_on_vector(t, n):
-    return n == 3 and t % 4 != 3
+GROUPS = [(first, 4) for first in range(0, 28, 4)] + [(28, 3), (31, 1)]
+FLOPS = 2 * ROWS * EXPERTS * HIDDEN * OUT_C
 
 
 def tile_tensormoe_pb_t_kernel(tc, h_pre, W_mo, weights_n, leak_n, out):
     nc = tc.nc
     with ExitStack() as ctx:
-        if PIN:
-            ctx.enter_context(tc.manual_schedule())
+        ctx.enter_context(tc.manual_schedule())
         const = ctx.enter_context(tc.tile_pool(name="const", bufs=1))
         work = ctx.enter_context(tc.tile_pool(name="work", bufs=2))
-        xpsum = ctx.enter_context(tc.psum_pool(name="xpsum", bufs=XY_BUFS))
-        mpsum = xpsum
+        psum_x = ctx.enter_context(tc.psum_pool(name="psum_x", bufs=4))
+        psum_y = ctx.enter_context(tc.psum_pool(name="psum_y", bufs=2))
+        psum_m = ctx.enter_context(tc.psum_pool(name="psum_m", bufs=1))
 
-        h_view = h_pre.rearrange("(p t) n m -> p t (n m)", t=NT)
-        out_view = out.rearrange("(p t) o -> p t o", t=NT)
+        h_view = h_pre.rearrange("(p t) n m -> p t (n m)", t=TILES)
+        out_view = out.rearrange("(p t) o -> p t o", t=TILES)
 
-        lkb = const.tile([P, HN], BF16)
-        nc.sync.dma_start(out=lkb[:], in_=leak_n.partition_broadcast(P))
-        wtb = const.tile([P, NT * HN], BF16)
-        nc.sync.dma_start(out=wtb[:], in_=weights_n.rearrange("(p t) n -> p (t n)", t=NT))
+        leak_bf = const.tile([P, EXPERTS], BF16)
+        nc.sync.dma_start(out=leak_bf[:], in_=leak_n.partition_broadcast(P))
+        routing_bf = const.tile([P, TILES * EXPERTS], BF16)
+        nc.sync.dma_start(out=routing_bf[:], in_=weights_n.rearrange("(p t) n -> p (t n)", t=TILES))
 
-        H = {}
-        X = {}
-        L = {}
-        G = {}
-        Q = {}
-        Y = {}
-        Z = {}
-        C = {}
-        C2 = {}
-        MA = {}
-        MB = {}
-        TT = {}
-        U = {}
-        FIN = {}
-        UC = {}
+        h_tiles = {}
 
-        def load(t, pieces):
-            hsb = work.tile([P, HN * HM], BF16, name="hsb", bufs=6)
-            w = HN * HM // pieces
-            for i in range(pieces):
-                nc.sync.dma_start(out=hsb[:, i * w : (i + 1) * w], in_=h_view[:, t, i * w : (i + 1) * w])
-            H[t] = hsb
+        def new_h_tile(t):
+            h_sb = work.tile([P, EXPERTS * HIDDEN], BF16, name="h_sb", bufs=6)
+            h_tiles[t] = h_sb
+            return h_sb
 
-        load(0, HN)
-        wraw = const.tile([P, 16 * 512], BF16)
-        nc.sync.dma_start(
-            out=wraw[:].rearrange("p (a r) -> p a r", a=16),
-            in_=W_mo.rearrange("n (g u p e) o -> p (n g u) (e o)", g=2, u=2, p=P, e=2),
-        )
+        def load(t):
+            nc.sync.dma_start(out=new_h_tile(t)[:], in_=h_view[:, t, :])
+
+        first_h = new_h_tile(0)
+        w_raw = const.tile([P, EXPERTS * 2048], BF16)
+        for n in range(EXPERTS):
+            nc.sync.dma_start(out=first_h[:, n * HIDDEN : (n + 1) * HIDDEN], in_=h_view[:, 0, n * HIDDEN : (n + 1) * HIDDEN])
+            nc.sync.dma_start(
+                out=w_raw[:, n * 2048 : (n + 1) * 2048].rearrange("p (a r) -> p a r", a=4),
+                in_=W_mo[n].rearrange("(g u p e) o -> p (g u) (e o)", g=PASSES, u=2, p=P, e=2),
+            )
         for t in range(1, AHEAD):
-            load(t, 1)
+            load(t)
 
         ident = const.tile([P, P], F32)
         make_identity(nc, ident[:])
-
         one = const.tile([P, 1], F32)
         nc.vector.memset(one[:], 1.0)
         warm = const.tile([P, 1], F32)
         nc.scalar.activation(out=warm[:], in_=one[:], func=ACT.Abs_reciprocal_sqrt)
 
-        lk = const.tile([P, HN], F32)
-        nc.vector.tensor_copy(out=lk[:], in_=lkb[:])
-        sg = const.tile([P, HN], F32)
-        nc.vector.tensor_scalar(out=sg[:], in0=lk[:], scalar1=1.0, scalar2=-2.0, op0=ALU.is_gt, op1=ALU.mult)
-        nc.vector.tensor_scalar_add(out=sg[:], in0=sg[:], scalar1=1.0)
-        wp = const.tile([P, NT, HN], F32)
+        leak = const.tile([P, EXPERTS], F32)
+        nc.vector.tensor_copy(out=leak[:], in_=leak_bf[:])
+        sign = const.tile([P, EXPERTS], F32)
+        nc.vector.tensor_scalar(out=sign[:], in0=leak[:], scalar1=1.0, scalar2=-2.0, op0=ALU.is_gt, op1=ALU.mult)
+        nc.vector.tensor_scalar_add(out=sign[:], in0=sign[:], scalar1=1.0)
+        routing = const.tile([P, TILES, EXPERTS], F32)
         nc.vector.tensor_tensor(
-            out=wp[:],
-            in0=wtb[:].rearrange("p (t n) -> p t n", n=HN),
-            in1=sg[:].unsqueeze(1).to_broadcast([P, NT, HN]),
+            out=routing[:],
+            in0=routing_bf[:].rearrange("p (t n) -> p t n", n=EXPERTS),
+            in1=sign[:].unsqueeze(1).to_broadcast([P, TILES, EXPERTS]),
             op=ALU.mult,
         )
-        wgrp = const.tile([P, 8192], BF16, align_bytes=64)
-        wcodes = const.tile([P, 2048], U32, align_bytes=64)
-        wscales = const.tile([P, 2048], U8, align_bytes=64)
-        su = const.tile([P, NT, HN], F32)
-        sq = const.tile([P, NT, HN], F32)
+        sum_u = const.tile([P, TILES, EXPERTS], F32)
+        sum_uu = const.tile([P, TILES, EXPERTS], F32)
 
-        wsrc = wraw[:].rearrange("p (a t o) -> p a o t", a=8, t=4, o=OC)
-        wdst = wgrp[:].rearrange("p (a o t) -> p a o t", a=8, t=4, o=OC)
+        w_grouped = const.tile([P, EXPERTS * 2048], BF16, align_bytes=64)
+        w_codes = const.tile([P, EXPERTS * 512], U32, align_bytes=64)
+        w_scales = const.tile([P, EXPERTS * 512], U8, align_bytes=64)
+        w_src = w_raw[:].rearrange("p (a t o) -> p a o t", a=EXPERTS * PASSES, t=4, o=OUT_C)
+        w_dst = w_grouped[:].rearrange("p (a o t) -> p a o t", a=EXPERTS * PASSES, t=4, o=OUT_C)
 
-        def w_regroup(a):
-            if a in W_ON_SCALAR:
-                nc.scalar.copy(out=wdst[:, a], in_=wsrc[:, a])
-            else:
-                nc.vector.tensor_copy(out=wdst[:, a], in_=wsrc[:, a])
+        def regroup_w(n):
+            nc.vector.tensor_copy(out=w_dst[:, PASSES * n], in_=w_src[:, PASSES * n])
+            nc.scalar.copy(out=w_dst[:, PASSES * n + 1], in_=w_src[:, PASSES * n + 1])
 
-        def w_quantise(n):
+        def quantise_w(n):
             nc.vector.quantize_mx(
-                out=wcodes[:, n * 512 : (n + 1) * 512].bitcast(FP8X4),
-                scales=wscales[:, n * 512 : (n + 1) * 512],
-                in_=wgrp[:, n * 2048 : (n + 1) * 2048],
+                out=w_codes[:, n * 512 : (n + 1) * 512].bitcast(FP8X4),
+                scales=w_scales[:, n * 512 : (n + 1) * 512],
+                in_=w_grouped[:, n * 2048 : (n + 1) * 2048],
             )
+
+        x_banks, leaked, grouped, h_codes = {}, {}, {}, {}
 
         def flip(s):
-            t, n = divmod(s, HN)
-            sl = H[t][:, n * HM : (n + 1) * HM]
-            nc.vector.tensor_scalar(out=sl, in0=sl, scalar1=sg[:, n : n + 1], scalar2=None, op0=ALU.mult)
+            t, n = divmod(s, EXPERTS)
+            x = h_tiles[t][:, n * HIDDEN : (n + 1) * HIDDEN]
+            nc.vector.tensor_scalar(out=x, in0=x, scalar1=sign[:, n : n + 1], scalar2=None, op0=ALU.mult)
 
         def transposes(s):
-            t, n = divmod(s, HN)
-            hw = H[t][:].bitcast(F32)
-            xt = xpsum.tile([P, 512], F32, name="xt", tag="xy")
+            t, n = divmod(s, EXPERTS)
+            words = h_tiles[t][:].bitcast(F32)
+            x_bank = psum_x.tile([P, 512], F32, name="x_bank")
             for u in range(2):
-                for g in range(2):
-                    j = u * 2 + g
-                    c0 = n * 512 + g * 256 + u * 128
-                    nc.tensor.transpose(xt[:, j * P : (j + 1) * P], hw[:, c0 : c0 + P], ident[:])
-            X[s] = xt
-            if n == HN - 1:
-                H.pop(t)
+                for g in range(PASSES):
+                    first = n * 512 + g * 256 + u * P
+                    quarter = (2 * u + g) * P
+                    nc.tensor.transpose(x_bank[:, quarter : quarter + P], words[:, first : first + P], ident[:])
+            x_banks[s] = x_bank
+            if n == EXPERTS - 1:
+                h_tiles.pop(t)
 
         def leak_times(s):
-            t, n = divmod(s, HN)
-            xb = X[s][:].bitcast(BF16)
-            lt = work.tile([P, HM], BF16, name="lt", bufs=4)
-            if l_on_vector(t, n):
-                nc.vector.tensor_scalar(out=lt[:], in0=xb, scalar1=lk[:, n : n + 1], scalar2=None, op0=ALU.mult)
+            t, n = divmod(s, EXPERTS)
+            x = x_banks[s][:].bitcast(BF16)
+            product = work.tile([P, HIDDEN], BF16, name="leaked", bufs=4)
+            if n == 3 and t % 4 != 3:
+                nc.vector.tensor_scalar(out=product[:], in0=x, scalar1=leak[:, n : n + 1], scalar2=None, op0=ALU.mult)
             else:
-                nc.scalar.activation(out=lt[:], in_=xb, func=ACT.Copy, scale=lk[:, n : n + 1])
-            L[s] = lt
+                nc.scalar.activation(out=product[:], in_=x, func=ACT.Copy, scale=leak[:, n : n + 1])
+            leaked[s] = product
 
         def take_max(s):
-            xb = X.pop(s)[:].bitcast(BF16)
-            lt = L.pop(s)
-            grp = work.tile([P, HM], BF16, name="grp", bufs=4, align_bytes=64)
+            x = x_banks.pop(s)[:].bitcast(BF16)
+            rectified = work.tile([P, HIDDEN], BF16, name="grouped", bufs=4, align_bytes=64)
             nc.vector.tensor_tensor(
-                out=grp[:].rearrange("p (w u e) -> p w u e", u=2, e=2),
-                in0=lt[:].rearrange("p (u w e) -> p w u e", u=2, e=2),
-                in1=xb.rearrange("p (u w e) -> p w u e", u=2, e=2),
+                out=rectified[:].rearrange("p (w u e) -> p w u e", u=2, e=2),
+                in0=leaked.pop(s)[:].rearrange("p (u w e) -> p w u e", u=2, e=2),
+                in1=x.rearrange("p (u w e) -> p w u e", u=2, e=2),
                 op=ALU.max,
             )
-            G[s] = grp
+            grouped[s] = rectified
 
         def quantise(s):
-            grp = G.pop(s)
             codes = work.tile([P, 256], U32, name="codes", bufs=8, align_bytes=64)
             scales = work.tile([P, 256], U8, name="scales", bufs=8, align_bytes=64)
-            nc.vector.quantize_mx(out=codes[:].bitcast(FP8X4), scales=scales[:], in_=grp[:])
-            Q[s] = (codes, scales)
+            nc.vector.quantize_mx(out=codes[:].bitcast(FP8X4), scales=scales[:], in_=grouped.pop(s)[:])
+            h_codes[s] = (codes, scales)
 
-        def mx(s):
-            t, n = divmod(s, HN)
-            codes, scales = Q.pop(s)
-            if n % 2 == 0:
-                y = xpsum.tile([P, 2, OC], F32, name="y", tag="xy")
-                Y[s // 2] = y
-            y = Y[s // 2]
-            for g in range(2):
-                a = n * 2 + g
-                nc.tensor.matmul_mx(
-                    out=y[:, n % 2, :],
-                    lhsT=codes[:, g * P : (g + 1) * P].bitcast(FP8X4),
-                    lhsT_scale=scales[:, g * P : (g + 1) * P],
-                    rhs=wcodes[:, a * OC : (a + 1) * OC].bitcast(FP8X4),
-                    rhs_scale=wscales[:, a * OC : (a + 1) * OC],
-                    start=(g == 0),
-                    stop=(g == 1),
-                )
+        products, weighted, centred, squares, mean_bank, rms_bank, turned, normed = {}, {}, {}, {}, {}, {}, {}, {}
 
-        def weigh(s):
-            t, n = divmod(s, HN)
-            if n == 0:
-                z = work.tile([P, HN, OC], F32, name="z", bufs=3)
-                Z[t] = z
-            y = Y[s // 2]
-            nc.scalar.activation(out=Z[t][:, n, :], in_=y[:, n % 2, :], func=ACT.Copy, scale=wp[:, t, n : n + 1])
-            if n % 2 == 1:
-                Y.pop(s // 2)
+        def multiply(t):
+            for half in range(2):
+                y = psum_y.tile([P, 2, OUT_C], F32, name="y")
+                products[(t, half)] = y
+                for n in (2 * half, 2 * half + 1):
+                    codes, scales = h_codes.pop(EXPERTS * t + n)
+                    for g in range(PASSES):
+                        a = n * PASSES + g
+                        nc.tensor.matmul_mx(
+                            out=y[:, n % 2, :],
+                            lhsT=codes[:, g * P : (g + 1) * P].bitcast(FP8X4),
+                            lhsT_scale=scales[:, g * P : (g + 1) * P],
+                            rhs=w_codes[:, a * OUT_C : (a + 1) * OUT_C].bitcast(FP8X4),
+                            rhs_scale=w_scales[:, a * OUT_C : (a + 1) * OUT_C],
+                            start=(g == 0),
+                            stop=(g == PASSES - 1),
+                        )
 
-        def sum_over_experts(src, tagname):
-            m = mpsum.tile([P, 512], F32, name=tagname, tag="xy")
-            for hf in range(2):
-                for n in range(HN):
+        def weigh(t, half):
+            if half == 0:
+                z = work.tile([P, EXPERTS, OUT_C], F32, name="z", bufs=3)
+                weighted[t] = z
+            y = products.pop((t, half))
+            for n in (2 * half, 2 * half + 1):
+                nc.scalar.activation(out=weighted[t][:, n, :], in_=y[:, n % 2, :], func=ACT.Copy, scale=routing[:, t, n : n + 1])
+
+        def sum_over_experts(src, name):
+            bank = psum_m.tile([P, 512], F32, name=name)
+            for half in range(2):
+                for n in range(EXPERTS):
                     nc.tensor.matmul(
-                        out=m[:, hf * P : (hf + 1) * P],
-                        lhsT=src[:, n, hf * P : (hf + 1) * P],
+                        out=bank[:, half * P : (half + 1) * P],
+                        lhsT=src[:, n, half * P : (half + 1) * P],
                         rhs=ident[:],
                         start=(n == 0),
-                        stop=(n == HN - 1),
+                        stop=(n == EXPERTS - 1),
                         is_transpose=True,
                     )
-            return m
+            return bank
 
-        def back(m, src_t):
-            for hf in range(2):
-                nc.tensor.transpose(m[:, 256 + hf * P : 256 + (hf + 1) * P], src_t[:, hf * P : (hf + 1) * P], ident[:])
+        def turn_back(bank, src):
+            for half in range(2):
+                nc.tensor.transpose(bank[:, 256 + half * P : 256 + (half + 1) * P], src[:, half * P : (half + 1) * P], ident[:])
 
-        def e_sum(t):
-            MA[t] = sum_over_experts(Z[t], "mA")
+        def sum_weighted(t):
+            mean_bank[t] = sum_over_experts(weighted[t], "mean_bank")
 
-        def e_nm(t):
-            nmt = work.tile([P, OC], F32, name="nmt")
-            nc.scalar.activation(out=nmt[:], in_=MA[t][:, 0:256], func=ACT.Copy, scale=-0.25)
-            TT[t] = nmt
+        def minus_mean(t):
+            negative = work.tile([P, OUT_C], F32, name="minus_mean")
+            nc.scalar.activation(out=negative[:], in_=mean_bank[t][:, 0:256], func=ACT.Copy, scale=-1.0 / EXPERTS)
+            turned[t] = negative
 
-        def e_nmback(t):
-            back(MA[t], TT.pop(t))
+        def mean_back(t):
+            turn_back(mean_bank[t], turned.pop(t))
 
-        def e_centre(t):
-            c = work.tile([P, HN, OC], F32, name="c", bufs=3)
-            nm = MA.pop(t)[:, 256:512]
+        def centre(t):
+            c = work.tile([P, EXPERTS, OUT_C], F32, name="c", bufs=3)
             nc.vector.tensor_tensor(
-                out=c[:], in0=Z.pop(t)[:], in1=nm.unsqueeze(1).to_broadcast([P, HN, OC]), op=ALU.add
+                out=c[:],
+                in0=weighted.pop(t)[:],
+                in1=mean_bank.pop(t)[:, 256:512].unsqueeze(1).to_broadcast([P, EXPERTS, OUT_C]),
+                op=ALU.add,
             )
-            C[t] = c
+            centred[t] = c
 
-        def e_square(t):
-            c2 = work.tile([P, HN, OC], F32, name="c2")
-            nc.scalar.activation(out=c2[:], in_=C[t][:], func=ACT.Square)
-            C2[t] = c2
+        def square(t):
+            cc = work.tile([P, EXPERTS, OUT_C], F32, name="cc")
+            nc.scalar.activation(out=cc[:], in_=centred[t][:], func=ACT.Square)
+            squares[t] = cc
 
-        def e_q(t):
-            MB[t] = sum_over_experts(C2.pop(t), "mB")
+        def sum_squares(t):
+            rms_bank[t] = sum_over_experts(squares.pop(t), "rms_bank")
 
-        def e_r(t):
-            rt = work.tile([P, OC], F32, name="rt")
-            nc.scalar.activation(out=rt[:], in_=MB[t][:, 0:256], func=ACT.Abs_reciprocal_sqrt, scale=0.25)
-            TT[t] = rt
+        def one_over_rms(t):
+            r = work.tile([P, OUT_C], F32, name="one_over_rms")
+            nc.scalar.activation(out=r[:], in_=rms_bank[t][:, 0:256], func=ACT.Abs_reciprocal_sqrt, scale=1.0 / EXPERTS)
+            turned[t] = r
 
-        def e_rback(t):
-            back(MB[t], TT.pop(t))
+        def rms_back(t):
+            turn_back(rms_bank[t], turned.pop(t))
 
-        def e_u(t, n):
-            if t not in U:
-                u = work.tile([P, HN, OC], F32, name="u", bufs=10)
-                U[t] = u
-                UC[t] = 0
+        def normalise(t):
+            u = work.tile([P, EXPERTS, OUT_C], F32, name="u", bufs=10)
+            for n in range(EXPERTS):
+                nc.vector.scalar_tensor_tensor(
+                    out=u[:, n, :], in0=rms_bank[t][:, 256:512], scalar=1.0e8, in1=centred[t][:, n, :],
+                    op0=ALU.min, op1=ALU.mult, accum_out=sum_u[:, t, n : n + 1],
+                )
+            normed[t] = u
+            rms_bank.pop(t)
+            centred.pop(t)
+
+        def sums_of_squares(t):
+            for n in range(EXPERTS):
+                unused = work.tile([P, OUT_C], F32, name="unused")
+                nc.scalar.activation(out=unused[:], in_=normed[t][:, n, :], func=ACT.Square, accum_out=sum_uu[:, t, n : n + 1])
+
+        closing = {}
+
+        def variances(first, size):
+            tiles = slice(first, first + size)
+            mu = work.tile([P, size, EXPERTS], F32, name="mu")
+            nc.vector.tensor_scalar_mul(out=mu[:], in0=sum_u[:, tiles, :], scalar1=1.0 / OUT_C)
+            mu_mu = work.tile([P, size, EXPERTS], F32, name="mu_mu")
+            nc.vector.tensor_tensor(out=mu_mu[:], in0=mu[:], in1=mu[:], op=ALU.mult)
+            var = work.tile([P, size, EXPERTS], F32, name="var")
             nc.vector.scalar_tensor_tensor(
-                out=U[t][:, n, :], in0=MB[t][:, 256:512], scalar=1.0e8, in1=C[t][:, n, :], op0=ALU.min, op1=ALU.mult,
-                accum_out=su[:, t, n : n + 1],
+                out=var[:], in0=sum_uu[:, tiles, :], scalar=1.0 / OUT_C, in1=mu_mu[:], op0=ALU.mult, op1=ALU.subtract
             )
-            UC[t] += 1
-            if UC[t] == HN:
-                MB.pop(t)
-                C.pop(t)
+            closing[first] = {"mu": mu, "var": var}
 
-        def e_usq(t, n):
-            junk = work.tile([P, OC], F32, name="junk")
-            nc.scalar.activation(out=junk[:], in_=U[t][:, n, :], func=ACT.Square, accum_out=sq[:, t, n : n + 1])
+        def roots(first, size):
+            root = work.tile([P, size, EXPERTS], F32, name="root")
+            nc.scalar.activation(out=root[:], in_=closing[first]["var"][:], func=ACT.Abs_reciprocal_sqrt)
+            closing[first]["root"] = root
 
-        def fin(gi, step):
-            t0, size = GROUPS[gi]
-            ts = slice(t0, t0 + size)
+        def coefficients(first, size):
+            parts = closing[first]
+            a = work.tile([P, size, EXPERTS], F32, name="a")
+            nc.vector.tensor_scalar(out=a[:], in0=parts["root"][:], scalar1=1.0e8, scalar2=1.0 / EXPERTS, op0=ALU.min, op1=ALU.mult)
+            a_mu = work.tile([P, size, EXPERTS], F32, name="a_mu")
+            nc.vector.scalar_tensor_tensor(out=a_mu[:], in0=parts["mu"][:], scalar=-1.0, in1=a[:], op0=ALU.mult, op1=ALU.mult)
+            factor = work.tile([P, size, 3], F32, name="factor")
+            nc.vector.tensor_tensor(
+                out=factor[:], in0=a[:, :, 0:3], in1=a[:, :, 3:4].to_broadcast([P, size, 3]), op=ALU.subtract
+            )
+            offset = work.tile([P, size], F32, name="offset")
+            nc.vector.tensor_reduce(out=offset[:], in_=a_mu[:], axis=AX.X, op=ALU.add)
+            result = work.tile([P, size, OUT_C], F32, name="result")
+            parts["factor"] = factor
+            parts["offset"] = offset
+            parts["result"] = result
 
-            def small(name):
-                return work.tile([P, size, HN], F32, name=name)
-
-            if step == 0:
-                mu = small("mu")
-                nc.vector.tensor_scalar_mul(out=mu[:], in0=su[:, ts, :], scalar1=1.0 / OC)
-                FIN[gi] = {"mu": mu}
-            f = FIN[gi]
-            if step == 1:
-                m2 = small("m2")
-                nc.vector.tensor_tensor(out=m2[:], in0=f["mu"][:], in1=f["mu"][:], op=ALU.mult)
-                f["m2"] = m2
-            if step == 2:
-                var = small("var")
-                nc.vector.scalar_tensor_tensor(
-                    out=var[:], in0=sq[:, ts, :], scalar=1.0 / OC, in1=f["m2"][:], op0=ALU.mult, op1=ALU.subtract
+        def first_term(first, size, k):
+            parts = closing[first]
+            term = work.tile([P, OUT_C], F32, name="term")
+            u0 = normed[first + k][:, 0, :]
+            if size == 4:
+                nc.scalar.activation(
+                    out=term[:], in_=u0, func=ACT.Identity, scale=parts["factor"][:, k, 0:1], bias=parts["offset"][:, k : k + 1]
                 )
-                f["var"] = var
-            if step == 3:
-                a = small("a")
-                nc.scalar.activation(out=a[:], in_=f["var"][:], func=ACT.Abs_reciprocal_sqrt)
-                f["a"] = a
-            if step == 4:
-                a4 = small("a4")
-                nc.vector.tensor_scalar(out=a4[:], in0=f["a"][:], scalar1=1.0e8, scalar2=0.25, op0=ALU.min, op1=ALU.mult)
-                f["a4"] = a4
-            if step == 5:
-                am = small("am")
-                nc.vector.scalar_tensor_tensor(
-                    out=am[:], in0=f["mu"][:], scalar=-1.0, in1=f["a4"][:], op0=ALU.mult, op1=ALU.mult
-                )
-                f["am"] = am
-                dl = work.tile([P, size, 3], F32, name="dl")
-                nc.vector.tensor_tensor(
-                    out=dl[:], in0=f["a4"][:, :, 0:3], in1=f["a4"][:, :, 3:4].to_broadcast([P, size, 3]), op=ALU.subtract
-                )
-                f["dl"] = dl
-            if step == 6:
-                nk = work.tile([P, size], F32, name="nk")
-                nc.vector.tensor_reduce(out=nk[:], in_=f["am"][:], axis=AX.X, op=ALU.add)
-                f["nk"] = nk
-                ob = work.tile([P, size, OC], F32, name="ob")
-                f["ob"] = ob
-
-        def fin_first(gi, k):
-            f = FIN[gi]
-            f0 = work.tile([P, OC], F32, name="f0")
-            if GROUPS[gi][1] < GROUP:
+            else:
                 nc.vector.tensor_scalar(
-                    out=f0[:], in0=U[GROUPS[gi][0] + k][:, 0, :], scalar1=f["dl"][:, k, 0:1], scalar2=f["nk"][:, k : k + 1],
+                    out=term[:], in0=u0, scalar1=parts["factor"][:, k, 0:1], scalar2=parts["offset"][:, k : k + 1],
                     op0=ALU.mult, op1=ALU.add,
                 )
-            else:
-                nc.scalar.activation(
-                    out=f0[:], in_=U[GROUPS[gi][0] + k][:, 0, :], func=ACT.Identity,
-                    scale=f["dl"][:, k, 0:1], bias=f["nk"][:, k : k + 1],
-                )
-            f[("f0", k)] = f0
+            parts[k] = term
 
-        def fin_rest(gi, k):
-            f = FIN[gi]
-            u = U.pop(GROUPS[gi][0] + k)
-            f1 = work.tile([P, OC], F32, name="f1")
+        def other_terms(first, size, k):
+            parts = closing[first]
+            u = normed.pop(first + k)
+            two = work.tile([P, OUT_C], F32, name="two_terms")
             nc.vector.scalar_tensor_tensor(
-                out=f1[:], in0=u[:, 1, :], scalar=f["dl"][:, k, 1:2], in1=f[("f0", k)][:], op0=ALU.mult, op1=ALU.add
+                out=two[:], in0=u[:, 1, :], scalar=parts["factor"][:, k, 1:2], in1=parts[k][:], op0=ALU.mult, op1=ALU.add
             )
             nc.vector.scalar_tensor_tensor(
-                out=f["ob"][:, k, :], in0=u[:, 2, :], scalar=f["dl"][:, k, 2:3], in1=f1[:], op0=ALU.mult, op1=ALU.add
+                out=parts["result"][:, k, :], in0=u[:, 2, :], scalar=parts["factor"][:, k, 2:3], in1=two[:], op0=ALU.mult, op1=ALU.add
             )
 
-        def fin_store(gi):
-            f = FIN.pop(gi)
-            t0, size = GROUPS[gi]
-            nc.sync.dma_start(out=out_view[:, t0 : t0 + size, :], in_=f["ob"][:])
+        def store(first, size):
+            nc.sync.dma_start(out=out_view[:, first : first + size, :], in_=closing.pop(first)["result"][:])
 
-        bank_stage = {
-            "flip": flip, "T": transposes, "L": leak_times, "max": take_max, "quant": quantise, "mx": mx, "weigh": weigh,
-        }
-        tile_stage = {
-            "sum": e_sum, "nm": e_nm, "nmb": e_nmback, "ce0": e_centre, "sq0": e_square, "qs": e_q, "r": e_r, "rb": e_rback,
-        }
+        def for_bank(stage, s):
+            if 0 <= s < BANKS:
+                stage(s)
 
-        events = {}
+        def for_tile(stage, steps_since_tile_0, *more):
+            t, rest = divmod(steps_since_tile_0, EXPERTS)
+            if rest == 0 and 0 <= t < TILES:
+                stage(t, *more)
 
-        def at(step, rank, sub, fn, args):
-            if step not in events:
-                events[step] = []
-            events[step].append((rank, sub, len(events[step]), fn, args))
-
-        def advance(s):
-            return min(ADV_MAX, max(0, (s - ADV_FROM) // ADV_EVERY))
-
-        for rank, (name, lag) in enumerate(ORDER):
-            if name in bank_stage:
-                for s in range(NS):
-                    adv = advance(s) if name in ADVANCED else 0
-                    at(s + lag[s % HN] - adv, rank, s, bank_stage[name], (s,))
-            elif name[0:2] == "wr":
-                at(lag, rank, 0, w_regroup, (int(name[2]),))
-            elif name[0:2] == "wq":
-                at(lag, rank, 0, w_quantise, (int(name[2]),))
-            elif name in tile_stage:
-                for t in range(NT):
-                    at(HN * t + lag, rank, t, tile_stage[name], (t,))
-            elif name[0:3] == "usq":
-                n = int(name[3])
-                for t in range(NT):
-                    at(HN * t + (lag if t < TAIL_FROM else (USQ_T0, USQ_T1, USQ_T2, USQ_T3)[n]), rank, t, e_usq, (t, n))
-            else:
-                for t in range(NT):
-                    at(HN * t + lag, rank, t, e_u, (t, int(name[1])))
-        flip_lag = [lag for name, lag in ORDER if name == "flip"][0]
-        for t in range(AHEAD, NT):
-            at(HN * t + flip_lag[0] - advance(HN * t) - HN * AHEAD, -1, t, load, (t, 1))
-        after = len(ORDER)
-        for gi in range(len(GROUPS)):
-            t0, size = GROUPS[gi]
-            base = HN * (t0 + size - GROUP) + FIN_BASE
-            if t0 >= TAIL_FROM:
-                base = HN * (t0 + size - 1) + (FIN_T0, FIN_T1, FIN_T2)[gi - len(GROUPS) + 3]
-            for step in range(7):
-                at(base + step, after, gi, fin, (gi, step))
-            for k in range(size):
-                at(base + 7 + k, after + 1, gi, fin_first, (gi, k))
-                at(base + 8 + k, after + 2, gi, fin_rest, (gi, k))
-            at(base + 9 + size, after + 3, gi, fin_store, (gi,))
-        for step in sorted(events):
-            for rank, sub, k, fn, args in sorted(events[step], key=lambda ev: ev[0:3]):
-                fn(*args)
+        last_step = EXPERTS * (TILES - 1) + 31
+        for step in range(last_step + 1):
+            for_tile(load, step + EXPERTS * AHEAD)
+            for_bank(flip, step)
+            for_bank(transposes, step - 2)
+            for_bank(leak_times, step - 3)
+            for_bank(take_max, step - 4)
+            for_bank(quantise, step - 6)
+            for_tile(multiply, step - 11)
+            for_tile(weigh, step - 12, 0)
+            for_tile(weigh, step - 13, 1)
+            for_tile(sum_weighted, step - 14)
+            for_tile(minus_mean, step - 15)
+            for_tile(mean_back, step - 16)
+            for_tile(centre, step - 17)
+            for_tile(square, step - 19)
+            for_tile(sum_squares, step - 21)
+            for_tile(one_over_rms, step - 22)
+            for_tile(rms_back, step - 23)
+            for_tile(normalise, step - 24)
+            for_tile(sums_of_squares, step - 25)
+            if 2 <= step < 2 + EXPERTS:
+                regroup_w(step - 2)
+            if 3 <= step < 3 + EXPERTS:
+                quantise_w(step - 3)
+            for first, size in GROUPS:
+                k = step - (EXPERTS * (first + size - 1) + 26)
+                if k == 0:
+                    variances(first, size)
+                if k == 1:
+                    roots(first, size)
+                if k == 2:
+                    coefficients(first, size)
+                if 3 <= k < 3 + size:
+                    first_term(first, size, k - 3)
+                if 4 <= k < 4 + size:
+                    other_terms(first, size, k - 4)
+                if k == 4 + size:
+                    store(first, size)

@@ -28,9 +28,7 @@ def tile_tensormoe_pb_t_kernel(tc, h_pre, W_mo, weights_n, leak_n, out):
         ctx.enter_context(tc.manual_schedule())
         const = ctx.enter_context(tc.tile_pool(name="const", bufs=1))
         work = ctx.enter_context(tc.tile_pool(name="work", bufs=2))
-        psum_x = ctx.enter_context(tc.psum_pool(name="psum_x", bufs=4))
-        psum_y = ctx.enter_context(tc.psum_pool(name="psum_y", bufs=2))
-        psum_m = ctx.enter_context(tc.psum_pool(name="psum_m", bufs=1))
+        psum = ctx.enter_context(tc.psum_pool(name="psum", bufs=8))
 
         h_view = h_pre.rearrange("(p t) n m -> p t (n m)", t=TILES)
         out_view = out.rearrange("(p t) o -> p t o", t=TILES)
@@ -110,7 +108,7 @@ def tile_tensormoe_pb_t_kernel(tc, h_pre, W_mo, weights_n, leak_n, out):
         def transposes(s):
             t, n = divmod(s, EXPERTS)
             words = h_tiles[t][:].bitcast(F32)
-            x_bank = psum_x.tile([P, 512], F32, name="x_bank")
+            x_bank = psum.tile([P, 512], F32, name="x_bank", tag="bank")
             for u in range(2):
                 for g in range(PASSES):
                     first = n * 512 + g * 256 + u * P
@@ -149,34 +147,34 @@ def tile_tensormoe_pb_t_kernel(tc, h_pre, W_mo, weights_n, leak_n, out):
 
         products, weighted, centred, squares, mean_bank, rms_bank, turned, normed = {}, {}, {}, {}, {}, {}, {}, {}
 
-        def multiply(t):
-            for half in range(2):
-                y = psum_y.tile([P, 2, OUT_C], F32, name="y")
-                products[(t, half)] = y
-                for n in (2 * half, 2 * half + 1):
-                    codes, scales = h_codes.pop(EXPERTS * t + n)
-                    for g in range(PASSES):
-                        a = n * PASSES + g
-                        nc.tensor.matmul_mx(
-                            out=y[:, n % 2, :],
-                            lhsT=codes[:, g * P : (g + 1) * P].bitcast(FP8X4),
-                            lhsT_scale=scales[:, g * P : (g + 1) * P],
-                            rhs=w_codes[:, a * OUT_C : (a + 1) * OUT_C].bitcast(FP8X4),
-                            rhs_scale=w_scales[:, a * OUT_C : (a + 1) * OUT_C],
-                            start=(g == 0),
-                            stop=(g == PASSES - 1),
-                        )
+        def multiply(s):
+            n = s % EXPERTS
+            if n % 2 == 0:
+                y = psum.tile([P, 2, OUT_C], F32, name="y", tag="bank")
+                products[s // 2] = y
+            codes, scales = h_codes.pop(s)
+            for g in range(PASSES):
+                a = n * PASSES + g
+                nc.tensor.matmul_mx(
+                    out=products[s // 2][:, n % 2, :],
+                    lhsT=codes[:, g * P : (g + 1) * P].bitcast(FP8X4),
+                    lhsT_scale=scales[:, g * P : (g + 1) * P],
+                    rhs=w_codes[:, a * OUT_C : (a + 1) * OUT_C].bitcast(FP8X4),
+                    rhs_scale=w_scales[:, a * OUT_C : (a + 1) * OUT_C],
+                    start=(g == 0),
+                    stop=(g == PASSES - 1),
+                )
 
-        def weigh(t, half):
-            if half == 0:
+        def weigh(s):
+            t, n = divmod(s, EXPERTS)
+            if n == 0:
                 z = work.tile([P, EXPERTS, OUT_C], F32, name="z", bufs=3)
                 weighted[t] = z
-            y = products.pop((t, half))
-            for n in (2 * half, 2 * half + 1):
-                nc.scalar.activation(out=weighted[t][:, n, :], in_=y[:, n % 2, :], func=ACT.Copy, scale=routing[:, t, n : n + 1])
+            y = products[s // 2] if n % 2 == 0 else products.pop(s // 2)
+            nc.scalar.activation(out=weighted[t][:, n, :], in_=y[:, n % 2, :], func=ACT.Copy, scale=routing[:, t, n : n + 1])
 
         def sum_over_experts(src, name):
-            bank = psum_m.tile([P, 512], F32, name=name)
+            bank = psum.tile([P, 512], F32, name=name, tag="bank")
             for half in range(2):
                 for n in range(EXPERTS):
                     nc.tensor.matmul(
@@ -230,21 +228,22 @@ def tile_tensormoe_pb_t_kernel(tc, h_pre, W_mo, weights_n, leak_n, out):
         def rms_back(t):
             turn_back(rms_bank[t], turned.pop(t))
 
-        def normalise(t):
-            u = work.tile([P, EXPERTS, OUT_C], F32, name="u", bufs=10)
-            for n in range(EXPERTS):
-                nc.vector.scalar_tensor_tensor(
-                    out=u[:, n, :], in0=rms_bank[t][:, 256:512], scalar=1.0e8, in1=centred[t][:, n, :],
-                    op0=ALU.min, op1=ALU.mult, accum_out=sum_u[:, t, n : n + 1],
-                )
-            normed[t] = u
+        def normalise(t, n):
+            if t not in normed:
+                u = work.tile([P, EXPERTS, OUT_C], F32, name="u", bufs=10)
+                normed[t] = u
+            nc.vector.scalar_tensor_tensor(
+                out=normed[t][:, n, :], in0=rms_bank[t][:, 256:512], scalar=1.0e8, in1=centred[t][:, n, :],
+                op0=ALU.min, op1=ALU.mult, accum_out=sum_u[:, t, n : n + 1],
+            )
+
+        def release(t):
             rms_bank.pop(t)
             centred.pop(t)
 
-        def sums_of_squares(t):
-            for n in range(EXPERTS):
-                unused = work.tile([P, OUT_C], F32, name="unused")
-                nc.scalar.activation(out=unused[:], in_=normed[t][:, n, :], func=ACT.Square, accum_out=sum_uu[:, t, n : n + 1])
+        def sum_of_squares(t, n):
+            unused = work.tile([P, OUT_C], F32, name="unused")
+            nc.scalar.activation(out=unused[:], in_=normed[t][:, n, :], func=ACT.Square, accum_out=sum_uu[:, t, n : n + 1])
 
         closing = {}
 
@@ -315,47 +314,59 @@ def tile_tensormoe_pb_t_kernel(tc, h_pre, W_mo, weights_n, leak_n, out):
             if 0 <= s < BANKS:
                 stage(s)
 
-        def for_tile(stage, steps_since_tile_0, *more):
+        def for_pair(stage, s):
+            if s % 2 == 0:
+                for_bank(stage, s)
+                for_bank(stage, s + 1)
+
+        def for_tile(stage, steps_since_tile_0, *expert):
             t, rest = divmod(steps_since_tile_0, EXPERTS)
             if rest == 0 and 0 <= t < TILES:
-                stage(t, *more)
+                stage(t, *expert)
 
-        last_step = EXPERTS * (TILES - 1) + 31
-        for step in range(last_step + 1):
+        for step in range(EXPERTS * (TILES - 1) + 43):
             for_tile(load, step + EXPERTS * AHEAD)
-            for_bank(flip, step)
-            for_bank(transposes, step - 2)
-            for_bank(leak_times, step - 3)
-            for_bank(take_max, step - 4)
-            for_bank(quantise, step - 6)
-            for_tile(multiply, step - 11)
-            for_tile(weigh, step - 12, 0)
-            for_tile(weigh, step - 13, 1)
-            for_tile(sum_weighted, step - 14)
-            for_tile(minus_mean, step - 15)
-            for_tile(mean_back, step - 16)
-            for_tile(centre, step - 17)
-            for_tile(square, step - 19)
-            for_tile(sum_squares, step - 21)
-            for_tile(one_over_rms, step - 22)
-            for_tile(rms_back, step - 23)
-            for_tile(normalise, step - 24)
-            for_tile(sums_of_squares, step - 25)
+            if 1 <= step < 1 + EXPERTS:
+                regroup_w(step - 1)
             if 2 <= step < 2 + EXPERTS:
-                regroup_w(step - 2)
-            if 3 <= step < 3 + EXPERTS:
-                quantise_w(step - 3)
+                quantise_w(step - 2)
+            for_tile(sum_squares, step - 21)
+            for_tile(sum_of_squares, step - 28, 1)
+            for_tile(sum_of_squares, step - 31, 0)
+            for_tile(mean_back, step - 18)
+            for_bank(transposes, step - 5)
+            for_pair(quantise, step - 9)
+            if step % 2 == 0:
+                for_bank(flip, step - 1)
+                for_bank(flip, step)
+            for_tile(centre, step - 18)
+            for_tile(normalise, step - 23, 3)
+            for_pair(leak_times, step - 7)
+            for_tile(sum_of_squares, step - 25, 3)
+            for_tile(normalise, step - 23, 2)
+            for_pair(multiply, step - 10)
+            for_tile(normalise, step - 23, 0)
+            for_tile(sum_of_squares, step - 26, 2)
+            for_bank(weigh, step - 11)
+            for_tile(square, step - 19)
+            for_tile(one_over_rms, step - 22)
+            for_bank(take_max, step - 7)
+            for_tile(rms_back, step - 22)
+            for_tile(minus_mean, step - 16)
+            for_tile(sum_weighted, step - 15)
+            for_tile(normalise, step - 23, 1)
+            for_tile(release, step - 23)
             for first, size in GROUPS:
-                k = step - (EXPERTS * (first + size - 1) + 26)
+                k = step - (EXPERTS * (first + size - 1) + 32)
                 if k == 0:
                     variances(first, size)
-                if k == 1:
+                if k == 3:
                     roots(first, size)
-                if k == 2:
+                if k == 4:
                     coefficients(first, size)
-                if 3 <= k < 3 + size:
-                    first_term(first, size, k - 3)
-                if 4 <= k < 4 + size:
-                    other_terms(first, size, k - 4)
-                if k == 4 + size:
+                if 7 <= k < 7 + size:
+                    first_term(first, size, k - 7)
+                if 8 <= k < 8 + size:
+                    other_terms(first, size, k - 8)
+                if k == 9 + size:
                     store(first, size)

from contextlib import ExitStack

import concourse.mybir as mybir
from concourse.masks import make_identity

F32 = mybir.dt.float32
BF16 = mybir.dt.bfloat16
U32 = mybir.dt.uint32
U8 = mybir.dt.uint8
FP8X4 = mybir.dt.float8_e4m3fn_x4
ALU = mybir.AluOpType
ACT = mybir.ActivationFunctionType
AX = mybir.AxisListType

P = 128
ROWS, EXPERTS, HIDDEN, OUT_C = 4096, 4, 1024, 256
TILES = ROWS // P
BANKS = TILES * EXPERTS
PASSES = HIDDEN // 512
AHEAD = 3
GROUPS = [(first, 4) for first in range(0, 28, 4)] + [(28, 3), (31, 1)]
FLOPS = 2 * ROWS * EXPERTS * HIDDEN * OUT_C


def tile_tensormoe_pb_t_kernel(tc, h_pre, W_mo, weights_n, leak_n, out):
    nc = tc.nc
    with ExitStack() as ctx:
        ctx.enter_context(tc.manual_schedule())
        const = ctx.enter_context(tc.tile_pool(name="const", bufs=1))
        work = ctx.enter_context(tc.tile_pool(name="work", bufs=2))
        psum = ctx.enter_context(tc.psum_pool(name="psum", bufs=8))

        h_view = h_pre.rearrange("(p t) n m -> p t (n m)", t=TILES)
        out_view = out.rearrange("(p t) o -> p t o", t=TILES)

        leak_bf = const.tile([P, EXPERTS], BF16)
        nc.sync.dma_start(out=leak_bf[:], in_=leak_n.partition_broadcast(P))
        routing_bf = const.tile([P, TILES * EXPERTS], BF16)
        nc.sync.dma_start(out=routing_bf[:], in_=weights_n.rearrange("(p t) n -> p (t n)", t=TILES))

        h_tiles = {}

        def new_h_tile(t):
            h_sb = work.tile([P, EXPERTS * HIDDEN], BF16, name="h_sb", bufs=6)
            h_tiles[t] = h_sb
            return h_sb

        def load(t):
            nc.sync.dma_start(out=new_h_tile(t)[:], in_=h_view[:, t, :])

        first_h = new_h_tile(0)
        w_raw = const.tile([P, EXPERTS * 2048], BF16)
        for n in range(EXPERTS):
            nc.sync.dma_start(out=first_h[:, n * HIDDEN : (n + 1) * HIDDEN], in_=h_view[:, 0, n * HIDDEN : (n + 1) * HIDDEN])
            nc.sync.dma_start(
                out=w_raw[:, n * 2048 : (n + 1) * 2048].rearrange("p (a r) -> p a r", a=4),
                in_=W_mo[n].rearrange("(g u p e) o -> p (g u) (e o)", g=PASSES, u=2, p=P, e=2),
            )
        for t in range(1, AHEAD):
            load(t)

        ident = const.tile([P, P], F32)
        make_identity(nc, ident[:])
        one = const.tile([P, 1], F32)
        nc.vector.memset(one[:], 1.0)
        warm = const.tile([P, 1], F32)
        nc.scalar.activation(out=warm[:], in_=one[:], func=ACT.Abs_reciprocal_sqrt)

        leak = const.tile([P, EXPERTS], F32)
        nc.vector.tensor_copy(out=leak[:], in_=leak_bf[:])
        sign = const.tile([P, EXPERTS], F32)
        nc.vector.tensor_scalar(out=sign[:], in0=leak[:], scalar1=1.0, scalar2=-2.0, op0=ALU.is_gt, op1=ALU.mult)
        nc.vector.tensor_scalar_add(out=sign[:], in0=sign[:], scalar1=1.0)
        routing = const.tile([P, TILES, EXPERTS], F32)
        nc.vector.tensor_tensor(
            out=routing[:],
            in0=routing_bf[:].rearrange("p (t n) -> p t n", n=EXPERTS),
            in1=sign[:].unsqueeze(1).to_broadcast([P, TILES, EXPERTS]),
            op=ALU.mult,
        )
        sum_u = const.tile([P, TILES, EXPERTS], F32)
        sum_uu = const.tile([P, TILES, EXPERTS], F32)

        w_grouped = const.tile([P, EXPERTS * 2048], BF16, align_bytes=64)
        w_codes = const.tile([P, EXPERTS * 512], U32, align_bytes=64)
        w_scales = const.tile([P, EXPERTS * 512], U8, align_bytes=64)
        w_src = w_raw[:].rearrange("p (a t o) -> p a o t", a=EXPERTS * PASSES, t=4, o=OUT_C)
        w_dst = w_grouped[:].rearrange("p (a o t) -> p a o t", a=EXPERTS * PASSES, t=4, o=OUT_C)

        def regroup_w(n):
            nc.vector.tensor_copy(out=w_dst[:, PASSES * n], in_=w_src[:, PASSES * n])
            nc.scalar.copy(out=w_dst[:, PASSES * n + 1], in_=w_src[:, PASSES * n + 1])

        def quantise_w(n):
            nc.vector.quantize_mx(
                out=w_codes[:, n * 512 : (n + 1) * 512].bitcast(FP8X4),
                scales=w_scales[:, n * 512 : (n + 1) * 512],
                in_=w_grouped[:, n * 2048 : (n + 1) * 2048],
            )

        x_banks, leaked, grouped, h_codes = {}, {}, {}, {}

        def flip(s):
            t, n = divmod(s, EXPERTS)
            x = h_tiles[t][:, n * HIDDEN : (n + 1) * HIDDEN]
            nc.vector.tensor_scalar(out=x, in0=x, scalar1=sign[:, n : n + 1], scalar2=None, op0=ALU.mult)

        def transposes(s):
            t, n = divmod(s, EXPERTS)
            words = h_tiles[t][:].bitcast(F32)
            x_bank = psum.tile([P, 512], F32, name="x_bank", tag="bank")
            for u in range(2):
                for g in range(PASSES):
                    first = n * 512 + g * 256 + u * P
                    quarter = (2 * u + g) * P
                    nc.tensor.transpose(x_bank[:, quarter : quarter + P], words[:, first : first + P], ident[:])
            x_banks[s] = x_bank
            if n == EXPERTS - 1:
                h_tiles.pop(t)

        def leak_times(s):
            t, n = divmod(s, EXPERTS)
            x = x_banks[s][:].bitcast(BF16)
            product = work.tile([P, HIDDEN], BF16, name="leaked", bufs=4)
            if n == 3 and t % 4 != 3:
                nc.vector.tensor_scalar(out=product[:], in0=x, scalar1=leak[:, n : n + 1], scalar2=None, op0=ALU.mult)
            else:
                nc.scalar.activation(out=product[:], in_=x, func=ACT.Copy, scale=leak[:, n : n + 1])
            leaked[s] = product

        def take_max(s):
            x = x_banks.pop(s)[:].bitcast(BF16)
            rectified = work.tile([P, HIDDEN], BF16, name="grouped", bufs=4, align_bytes=64)
            nc.vector.tensor_tensor(
                out=rectified[:].rearrange("p (w u e) -> p w u e", u=2, e=2),
                in0=leaked.pop(s)[:].rearrange("p (u w e) -> p w u e", u=2, e=2),
                in1=x.rearrange("p (u w e) -> p w u e", u=2, e=2),
                op=ALU.max,
            )
            grouped[s] = rectified

        def quantise(s):
            codes = work.tile([P, 256], U32, name="codes", bufs=8, align_bytes=64)
            scales = work.tile([P, 256], U8, name="scales", bufs=8, align_bytes=64)
            nc.vector.quantize_mx(out=codes[:].bitcast(FP8X4), scales=scales[:], in_=grouped.pop(s)[:])
            h_codes[s] = (codes, scales)

        products, weighted, centred, squares, mean_bank, rms_bank, turned, normed = {}, {}, {}, {}, {}, {}, {}, {}

        def multiply(s):
            n = s % EXPERTS
            if n % 2 == 0:
                y = psum.tile([P, 2, OUT_C], F32, name="y", tag="bank")
                products[s // 2] = y
            codes, scales = h_codes.pop(s)
            for g in range(PASSES):
                a = n * PASSES + g
                nc.tensor.matmul_mx(
                    out=products[s // 2][:, n % 2, :],
                    lhsT=codes[:, g * P : (g + 1) * P].bitcast(FP8X4),
                    lhsT_scale=scales[:, g * P : (g + 1) * P],
                    rhs=w_codes[:, a * OUT_C : (a + 1) * OUT_C].bitcast(FP8X4),
                    rhs_scale=w_scales[:, a * OUT_C : (a + 1) * OUT_C],
                    start=(g == 0),
                    stop=(g == PASSES - 1),
                )

        def weigh(s):
            t, n = divmod(s, EXPERTS)
            if n == 0:
                z = work.tile([P, EXPERTS, OUT_C], F32, name="z", bufs=3)
                weighted[t] = z
            y = products[s // 2] if n % 2 == 0 else products.pop(s // 2)
            nc.scalar.activation(out=weighted[t][:, n, :], in_=y[:, n % 2, :], func=ACT.Copy, scale=routing[:, t, n : n + 1])

        def sum_over_experts(src, name):
            bank = psum.tile([P, 512], F32, name=name, tag="bank")
            for half in range(2):
                for n in range(EXPERTS):
                    nc.tensor.matmul(
                        out=bank[:, half * P : (half + 1) * P],
                        lhsT=src[:, n, half * P : (half + 1) * P],
                        rhs=ident[:],
                        start=(n == 0),
                        stop=(n == EXPERTS - 1),
                        is_transpose=True,
                    )
            return bank

        def turn_back(bank, src):
            for half in range(2):
                nc.tensor.transpose(bank[:, 256 + half * P : 256 + (half + 1) * P], src[:, half * P : (half + 1) * P], ident[:])

        def sum_weighted(t):
            mean_bank[t] = sum_over_experts(weighted[t], "mean_bank")

        def minus_mean(t):
            negative = work.tile([P, OUT_C], F32, name="minus_mean")
            nc.scalar.activation(out=negative[:], in_=mean_bank[t][:, 0:256], func=ACT.Copy, scale=-1.0 / EXPERTS)
            turned[t] = negative

        def mean_back(t):
            turn_back(mean_bank[t], turned.pop(t))

        def centre(t):
            c = work.tile([P, EXPERTS, OUT_C], F32, name="c", bufs=3)
            nc.vector.tensor_tensor(
                out=c[:],
                in0=weighted.pop(t)[:],
                in1=mean_bank.pop(t)[:, 256:512].unsqueeze(1).to_broadcast([P, EXPERTS, OUT_C]),
                op=ALU.add,
            )
            centred[t] = c

        def square(t):
            cc = work.tile([P, EXPERTS, OUT_C], F32, name="cc")
            nc.scalar.activation(out=cc[:], in_=centred[t][:], func=ACT.Square)
            squares[t] = cc

        def sum_squares(t):
            rms_bank[t] = sum_over_experts(squares.pop(t), "rms_bank")

        def one_over_rms(t):
            r = work.tile([P, OUT_C], F32, name="one_over_rms")
            nc.scalar.activation(out=r[:], in_=rms_bank[t][:, 0:256], func=ACT.Abs_reciprocal_sqrt, scale=1.0 / EXPERTS)
            turned[t] = r

        def rms_back(t):
            turn_back(rms_bank[t], turned.pop(t))

        def normalise(t, n):
            if t not in normed:
                u = work.tile([P, EXPERTS, OUT_C], F32, name="u", bufs=10)
                normed[t] = u
            nc.vector.scalar_tensor_tensor(
                out=normed[t][:, n, :], in0=rms_bank[t][:, 256:512], scalar=1.0e8, in1=centred[t][:, n, :],
                op0=ALU.min, op1=ALU.mult, accum_out=sum_u[:, t, n : n + 1],
            )

        def release(t):
            rms_bank.pop(t)
            centred.pop(t)

        def sum_of_squares(t, n):
            unused = work.tile([P, OUT_C], F32, name="unused")
            nc.scalar.activation(out=unused[:], in_=normed[t][:, n, :], func=ACT.Square, accum_out=sum_uu[:, t, n : n + 1])

        closing = {}

        def variances(first, size):
            tiles = slice(first, first + size)
            mu = work.tile([P, size, EXPERTS], F32, name="mu")
            nc.vector.tensor_scalar_mul(out=mu[:], in0=sum_u[:, tiles, :], scalar1=1.0 / OUT_C)
            mu_mu = work.tile([P, size, EXPERTS], F32, name="mu_mu")
            nc.vector.tensor_tensor(out=mu_mu[:], in0=mu[:], in1=mu[:], op=ALU.mult)
            var = work.tile([P, size, EXPERTS], F32, name="var")
            nc.vector.scalar_tensor_tensor(
                out=var[:], in0=sum_uu[:, tiles, :], scalar=1.0 / OUT_C, in1=mu_mu[:], op0=ALU.mult, op1=ALU.subtract
            )
            closing[first] = {"mu": mu, "var": var}

        def roots(first, size):
            root = work.tile([P, size, EXPERTS], F32, name="root")
            nc.scalar.activation(out=root[:], in_=closing[first]["var"][:], func=ACT.Abs_reciprocal_sqrt)
            closing[first]["root"] = root

        def coefficients(first, size):
            parts = closing[first]
            a = work.tile([P, size, EXPERTS], F32, name="a")
            nc.vector.tensor_scalar(out=a[:], in0=parts["root"][:], scalar1=1.0e8, scalar2=1.0 / EXPERTS, op0=ALU.min, op1=ALU.mult)
            a_mu = work.tile([P, size, EXPERTS], F32, name="a_mu")
            nc.vector.scalar_tensor_tensor(out=a_mu[:], in0=parts["mu"][:], scalar=-1.0, in1=a[:], op0=ALU.mult, op1=ALU.mult)
            factor = work.tile([P, size, 3], F32, name="factor")
            nc.vector.tensor_tensor(
                out=factor[:], in0=a[:, :, 0:3], in1=a[:, :, 3:4].to_broadcast([P, size, 3]), op=ALU.subtract
            )
            offset = work.tile([P, size], F32, name="offset")
            nc.vector.tensor_reduce(out=offset[:], in_=a_mu[:], axis=AX.X, op=ALU.add)
            result = work.tile([P, size, OUT_C], F32, name="result")
            parts["factor"] = factor
            parts["offset"] = offset
            parts["result"] = result

        def first_term(first, size, k):
            parts = closing[first]
            term = work.tile([P, OUT_C], F32, name="term")
            u0 = normed[first + k][:, 0, :]
            if size == 4:
                nc.scalar.activation(
                    out=term[:], in_=u0, func=ACT.Identity, scale=parts["factor"][:, k, 0:1], bias=parts["offset"][:, k : k + 1]
                )
            else:
                nc.vector.tensor_scalar(
                    out=term[:], in0=u0, scalar1=parts["factor"][:, k, 0:1], scalar2=parts["offset"][:, k : k + 1],
                    op0=ALU.mult, op1=ALU.add,
                )
            parts[k] = term

        def other_terms(first, size, k):
            parts = closing[first]
            u = normed.pop(first + k)
            two = work.tile([P, OUT_C], F32, name="two_terms")
            nc.vector.scalar_tensor_tensor(
                out=two[:], in0=u[:, 1, :], scalar=parts["factor"][:, k, 1:2], in1=parts[k][:], op0=ALU.mult, op1=ALU.add
            )
            nc.vector.scalar_tensor_tensor(
                out=parts["result"][:, k, :], in0=u[:, 2, :], scalar=parts["factor"][:, k, 2:3], in1=two[:], op0=ALU.mult, op1=ALU.add
            )

        def store(first, size):
            nc.sync.dma_start(out=out_view[:, first : first + size, :], in_=closing.pop(first)["result"][:])

        def for_bank(stage, s):
            if 0 <= s < BANKS:
                stage(s)

        def for_pair(stage, s):
            if s % 2 == 0:
                for_bank(stage, s)
                for_bank(stage, s + 1)

        def for_tile(stage, steps_since_tile_0, *expert):
            t, rest = divmod(steps_since_tile_0, EXPERTS)
            if rest == 0 and 0 <= t < TILES:
                stage(t, *expert)

        for step in range(EXPERTS * (TILES - 1) + 43):
            for_tile(load, step + EXPERTS * AHEAD)
            if 1 <= step < 1 + EXPERTS:
                regroup_w(step - 1)
            if 2 <= step < 2 + EXPERTS:
                quantise_w(step - 2)
            for_tile(sum_squares, step - 21)
            for_tile(sum_of_squares, step - 28, 1)
            for_tile(sum_of_squares, step - 31, 0)
            for_tile(mean_back, step - 18)
            for_bank(transposes, step - 5)
            for_pair(quantise, step - 9)
            if step % 2 == 0:
                for_bank(flip, step - 1)
                for_bank(flip, step)
            for_tile(centre, step - 18)
            for_tile(normalise, step - 23, 3)
            for_pair(leak_times, step - 7)
            for_tile(sum_of_squares, step - 25, 3)
            for_tile(normalise, step - 23, 2)
            for_pair(multiply, step - 10)
            for_tile(normalise, step - 23, 0)
            for_tile(sum_of_squares, step - 26, 2)
            for_bank(weigh, step - 11)
            for_tile(square, step - 19)
            for_tile(one_over_rms, step - 22)
            for_bank(take_max, step - 7)
            for_tile(rms_back, step - 22)
            for_tile(minus_mean, step - 16)
            for_tile(sum_weighted, step - 15)
            for_tile(normalise, step - 23, 1)
            for_tile(release, step - 23)
            for first, size in GROUPS:
                k = step - (EXPERTS * (first + size - 1) + 32)
                if k == 0:
                    variances(first, size)
                if k == 3:
                    roots(first, size)
                if k == 4:
                    coefficients(first, size)
                if 7 <= k < 7 + size:
                    first_term(first, size, k - 7)
                if 8 <= k < 8 + size:
                    other_terms(first, size, k - 8)
                if k == 9 + size:
                    store(first, size)
